import numpy as np
import ml_dtypes


def mxq(x, axis, fmt="e4m3"):
    dtype, down = {"e4m3": (ml_dtypes.float8_e4m3fn, 7), "e5m2": (ml_dtypes.float8_e5m2, 14)}[fmt]
    v = np.moveaxis(np.asarray(x, np.float32).astype(ml_dtypes.bfloat16).astype(np.float64), axis, -1)
    blocks = v.reshape(v.shape[:-1] + (-1, 32))
    amax = np.abs(blocks).max(-1, keepdims=True)
    byte = np.maximum(np.where(amax > 0, np.frexp(amax)[1] - 1 + 127, 0) - down, 1)
    scale = np.exp2(byte - 127.0)
    codes = (blocks / scale).astype(np.float32).astype(dtype).astype(np.float64)
    return np.moveaxis((codes * scale).reshape(v.shape), -1, axis)


WIDE = False


def mx_kscale(k):
    if not WIDE:
        return np.ones(k)
    levels = np.array([10, -10, 5, -5, 0])
    a = np.random.permutation(np.resize(levels, k // 512 * 4)).reshape(k // 512, 4)
    idx = np.arange(k)
    return np.exp2(a[idx // 512, idx % 128 // 32])


BF16 = ml_dtypes.bfloat16


def bf(x):
    return np.asarray(x, np.float32).astype(BF16)


def f64(x):
    return np.asarray(x).astype(np.float64)


B, P, WS, D, H = 2, 24, 8, 1024, 16
HD = D // H
WN = P // WS
N = WS * WS
SHIFT = WS // 2
LN_EPS = 1e-5


def layer_norm(x, g, b):
    mu = x.mean(-1, keepdims=True)
    var = x.var(-1, keepdims=True)
    return (x - mu) / np.sqrt(var + LN_EPS) * g + b


def window_partition(img):
    x = img.reshape(B, WN, WS, WN, WS, D).transpose(0, 1, 3, 2, 4, 5)
    return x.reshape(B * WN * WN, N, D)


def heads(t):
    return t.reshape(B * WN * WN, N, H, HD).transpose(0, 2, 1, 3)


def setup_inputs():
    s = mx_kscale(D)
    x_mid = np.random.standard_normal((B, P * P, D)) * 1.4 + np.random.standard_normal((B, P * P, 1)) * 0.5
    return {"x_mid": bf(x_mid),
            "g3": bf((1.0 + 0.1 * np.random.standard_normal(D)) * s),
            "b3": bf(0.1 * np.random.standard_normal(D) * s),
            "Wqkv2": bf(np.random.standard_normal((D, 3 * D)) / np.sqrt(D) / s[:, None]),
            "bqkv2": bf(0.1 * np.random.standard_normal(3 * D))}


def reference(x_mid, g3, b3, Wqkv2, bqkv2):
    h = layer_norm(f64(x_mid), f64(g3), f64(b3))
    img = np.roll(h.reshape(B, P, P, D), (SHIFT, SHIFT), axis=(1, 2))
    w = window_partition(img)
    qkv = (mxq(w, 2, "e4m3") @ mxq(f64(Wqkv2), 0, "e4m3")) + f64(bqkv2)
    q, k, v = np.split(qkv, 3, axis=-1)
    return heads(q), heads(k), heads(v)

@@ -1,0 +1,250 @@
+from contextlib import ExitStack
+
+import concourse.mybir as mybir
+from concourse.masks import make_identity
+
+FP8X4 = mybir.dt.float8_e4m3fn_x4
+BF16 = mybir.dt.bfloat16
+F32 = mybir.dt.float32
+U32 = mybir.dt.uint32
+U8 = mybir.dt.uint8
+ACT = mybir.ActivationFunctionType
+ALU = mybir.AluOpType
+
+P = 128
+IMAGES = 2
+SIDE = 24
+PATCHES = SIDE * SIDE
+WINDOW = 8
+SHIFT = 4
+GRID = SIDE // WINDOW
+POSITIONS = GRID * GRID
+D = 1024
+HEADS = 16
+HEAD_DIM = 64
+TENSORS = 3
+LN_EPS = 1e-5
+
+PACK = 4
+PASSES = D // (P * PACK)
+K_BLOCKS = D // P
+N_TILE = 512
+TOKEN_TILES = IMAGES * PATCHES // P
+TILES_PER_ROUND = 3
+ROUNDS = TOKEN_TILES // TILES_PER_ROUND
+STATS_CHUNK = 512
+
+RUN = 2
+
+FLOPS = 2 * IMAGES * PATCHES * D * TENSORS * D
+
+
+def cyclic_pieces(first, count, period):
+    start = first % period
+    head = min(count, period - start)
+    pieces = [(0, start, head)]
+    if head < count:
+        pieces.append((head, 0, count - head))
+    return pieces
+
+
+def window_groups():
+    groups = []
+    position = 0
+    while position < POSITIONS:
+        size = RUN if position + RUN <= POSITIONS else 1
+        groups.append((position, size))
+        position += size
+    return groups
+
+
+def tile_successiveswintransfomerblock_pa_kernel(
+    tc, x_mid, g3, b3, Wqkv2, bqkv2, out_0, out_1, out_2
+):
+    nc = tc.nc
+    outs = [out_0, out_1, out_2]
+    groups = window_groups()
+
+    with ExitStack() as stack:
+        keep = stack.enter_context(tc.tile_pool(name="keep", bufs=1))
+        x_pool = stack.enter_context(tc.tile_pool(name="x_pool", bufs=ROUNDS))
+        small = stack.enter_context(tc.tile_pool(name="small", bufs=ROUNDS))
+        z_pool = stack.enter_context(tc.tile_pool(name="z_pool", bufs=3))
+        w_pool = stack.enter_context(tc.tile_pool(name="w_pool", bufs=TENSORS * PASSES))
+        wg_pool = stack.enter_context(tc.tile_pool(name="wg_pool", bufs=4))
+        stage_pool = stack.enter_context(tc.tile_pool(name="stage_pool", bufs=4))
+        psum = stack.enter_context(tc.psum_pool(name="psum", bufs=8))
+
+        x_rounds = []
+        for r in range(ROUNDS):
+            x_round = x_pool.tile([P, TILES_PER_ROUND, D], BF16, name="x_round")
+            for b in range(IMAGES):
+                tiles = x_mid[b].rearrange("(a i) k -> i a k", i=P // IMAGES)
+                nc.sync.dma_start(
+                    out=x_round[b:P:IMAGES, :, :],
+                    in_=tiles[:, r * TILES_PER_ROUND : (r + 1) * TILES_PER_ROUND, :],
+                )
+            x_rounds.append(x_round)
+
+        gb_rows = keep.tile([P, P], BF16)
+        nc.vector.memset(gb_rows[:], 0.0)
+        nc.scalar.dma_start(out=gb_rows[0:K_BLOCKS, :], in_=g3.rearrange("(r c) -> r c", c=P))
+        nc.scalar.dma_start(
+            out=gb_rows[K_BLOCKS : 2 * K_BLOCKS, :], in_=b3.rearrange("(r c) -> r c", c=P)
+        )
+
+        w_rows = Wqkv2.rearrange("(c t p) n -> c p t n", t=PACK, p=P)
+        w_raw = {}
+        bias_bc = keep.tile([P, TENSORS * D], BF16)
+        for tensor in range(TENSORS):
+            for c in range(PASSES):
+                raw = w_pool.tile([P, PACK, D], BF16, name="w_raw")
+                nc.sync.dma_start(out=raw[:], in_=w_rows[c][:, :, tensor * D : (tensor + 1) * D])
+                w_raw[(tensor, c)] = raw
+            if tensor == 0:
+                nc.sync.dma_start(out=bias_bc[:], in_=bqkv2.partition_broadcast(P))
+
+        ident = keep.tile([P, P], F32)
+        make_identity(nc, ident[:])
+        gb_rows_f32 = keep.tile([P, P], F32)
+        nc.vector.tensor_copy(out=gb_rows_f32[:], in_=gb_rows[:])
+        gb_bank = psum.tile([P, N_TILE], F32, tag="bank")
+        nc.tensor.transpose(out=gb_bank[:, 0:P], in_=gb_rows_f32[:], identity=ident[:])
+        gb_cols = keep.tile([P, 2 * K_BLOCKS], F32)
+        nc.vector.tensor_copy(out=gb_cols[:], in_=gb_bank[:, 0 : 2 * K_BLOCKS])
+
+        planes = keep.tile([P, K_BLOCKS, IMAGES * PATCHES], BF16)
+        for r in range(ROUNDS):
+            x_round = x_rounds[r]
+            stats = small.tile([P, TILES_PER_ROUND, D // STATS_CHUNK, 6], F32)
+            mean_var = small.tile([P, TILES_PER_ROUND, 2], F32)
+            for a in range(TILES_PER_ROUND):
+                for h in range(D // STATS_CHUNK):
+                    nc.vector.bn_stats(
+                        out=stats[:, a, h, :],
+                        in_=x_round[:, a, h * STATS_CHUNK : (h + 1) * STATS_CHUNK],
+                    )
+                nc.vector.bn_aggr(
+                    out=mean_var[:, a, :], in_=stats[:, a, :, :].rearrange("p h s -> p (h s)")
+                )
+            std = small.tile([P, TILES_PER_ROUND], F32)
+            nc.scalar.activation(out=std[:], in_=mean_var[:, :, 1], func=ACT.Sqrt, bias=LN_EPS)
+            rstd = small.tile([P, TILES_PER_ROUND], F32)
+            nc.vector.reciprocal(out=rstd[:], in_=std[:])
+            shift = small.tile([P, TILES_PER_ROUND], F32)
+            nc.vector.scalar_tensor_tensor(
+                out=shift[:], in0=mean_var[:, :, 0], scalar=-1.0, in1=rstd[:],
+                op0=ALU.mult, op1=ALU.mult,
+            )
+
+            banks = [
+                psum.tile([P, N_TILE], F32, name="bank%d" % j, tag="bank") for j in range(K_BLOCKS)
+            ]
+            for a in range(TILES_PER_ROUND):
+                z = z_pool.tile([P, D], F32)
+                nc.scalar.activation(
+                    out=z[:], in_=x_round[:, a, :], func=ACT.Identity,
+                    scale=rstd[:, a : a + 1], bias=shift[:, a : a + 1],
+                )
+                for j in range(K_BLOCKS):
+                    nc.tensor.transpose(
+                        out=banks[j][:, a * P : (a + 1) * P],
+                        in_=z[:, j * P : (j + 1) * P],
+                        identity=ident[:],
+                    )
+            width = TILES_PER_ROUND * P
+            for j in range(K_BLOCKS):
+                nc.scalar.activation(
+                    out=planes[:, j, r * width : (r + 1) * width], in_=banks[j][:, 0:width],
+                    func=ACT.Identity,
+                    scale=gb_cols[:, j : j + 1], bias=gb_cols[:, K_BLOCKS + j : K_BLOCKS + j + 1],
+                )
+
+        x_grouped = keep.tile([P, PASSES, TOKEN_TILES * P, PACK], BF16, align_bytes=64)
+        x_codes = keep.tile([P, PASSES, TOKEN_TILES * P], U32, align_bytes=64)
+        x_scales = keep.tile([P, PASSES, TOKEN_TILES * P], U8, align_bytes=64)
+        for first, size in groups:
+            for c in range(PASSES):
+                image = planes[:, c * PACK : (c + 1) * PACK, :].rearrange(
+                    "p t (r c b) -> p r c b t", r=SIDE, c=SIDE, b=IMAGES
+                )
+                for g in range(size):
+                    tile_cols = x_grouped[:, c, (first + g) * P : (first + g + 1) * P, :].rearrange(
+                        "p (i q x b) t -> p i q x b t", i=WINDOW, x=size, b=IMAGES
+                    )
+                    for x in range(size):
+                        window_row, window_col = divmod(first + x, GRID)
+                        for i0, r0, rows in cyclic_pieces(window_row * WINDOW - SHIFT, WINDOW, SIDE):
+                            for j0, c0, cols in cyclic_pieces(
+                                window_col * WINDOW - SHIFT, WINDOW, SIDE
+                            ):
+                                nc.vector.tensor_copy(
+                                    out=tile_cols[
+                                        :, i0 : i0 + rows, j0 // size : (j0 + cols) // size, x, :, :
+                                    ],
+                                    in_=image[:, r0 : r0 + rows, c0 + g : c0 + cols : size, :, :],
+                                )
+            for c in range(PASSES):
+                cols = slice(first * P, (first + size) * P)
+                nc.vector.quantize_mx(
+                    out=x_codes[:, c, cols].bitcast(FP8X4),
+                    scales=x_scales[:, c, cols],
+                    in_=x_grouped[:, c, cols, :].rearrange("p m t -> p (m t)"),
+                )
+
+        w_codes = keep.tile([P, PASSES, TENSORS * D], U32, align_bytes=64)
+        w_scales = keep.tile([P, PASSES, TENSORS * D], U8, align_bytes=64)
+
+        def quantise_weights(tensor):
+            for half in range(D // N_TILE):
+                for c in range(PASSES):
+                    rows = w_raw[(tensor, c)][:, :, half * N_TILE : (half + 1) * N_TILE]
+                    grouped = wg_pool.tile([P, N_TILE, PACK], BF16, name="w_grouped", align_bytes=64)
+                    nc.scalar.copy(
+                        out=grouped[:].rearrange("p (n i) t -> p n t i", i=4),
+                        in_=rows.rearrange("p t (n i) -> p n t i", i=4),
+                    )
+                    cols = slice(tensor * D + half * N_TILE, tensor * D + (half + 1) * N_TILE)
+                    nc.vector.quantize_mx(
+                        out=w_codes[:, c, cols].bitcast(FP8X4),
+                        scales=w_scales[:, c, cols],
+                        in_=grouped[:].rearrange("p n t -> p (n t)"),
+                    )
+
+        quantise_weights(0)
+        for tensor in range(TENSORS):
+            if tensor + 1 < TENSORS:
+                quantise_weights(tensor + 1)
+            for first, size in groups:
+                stage = stage_pool.tile([P, HEADS, size, HEAD_DIM], F32, name="stage", tag="stage")
+                for g in range(size):
+                    tokens = slice((first + g) * P, (first + g + 1) * P)
+                    for half in range(D // N_TILE):
+                        cols = slice(tensor * D + half * N_TILE, tensor * D + (half + 1) * N_TILE)
+                        acc = psum.tile([P, N_TILE], F32, name="acc", tag="bank")
+                        for c in range(PASSES):
+                            nc.tensor.matmul_mx(
+                                out=acc[:],
+                                lhsT=x_codes[:, c, tokens].bitcast(FP8X4),
+                                lhsT_scale=x_scales[:, c, tokens],
+                                rhs=w_codes[:, c, cols].bitcast(FP8X4),
+                                rhs_scale=w_scales[:, c, cols],
+                                start=(c == 0),
+                                stop=(c == PASSES - 1),
+                            )
+                        heads = slice(half * N_TILE // HEAD_DIM, (half + 1) * N_TILE // HEAD_DIM)
+                        nc.vector.tensor_tensor(
+                            out=stage[:, heads, g, :],
+                            in0=acc[:].rearrange("p (h d) -> p h d", d=HEAD_DIM),
+                            in1=bias_bc[:, cols].rearrange("p (h d) -> p h d", d=HEAD_DIM),
+                            op=ALU.add,
+                        )
+                for x in range(size):
+                    for b in range(IMAGES):
+                        window = b * POSITIONS + first + x
+                        nc.sync.dma_start(
+                            out=outs[tensor][window].rearrange("h (j g) d -> j h (g d)", g=size),
+                            in_=stage[IMAGES * x + b : P : IMAGES * size].rearrange(
+                                "p h g d -> p h (g d)"
+                            ),
+                        )

@@ -34,7 +34,7 @@ TILES_PER_ROUND = 3
 ROUNDS = TOKEN_TILES // TILES_PER_ROUND
 STATS_CHUNK = 512
 
-RUN = 2
+RUN = 4
 
 FLOPS = 2 * IMAGES * PATCHES * D * TENSORS * D
 
@@ -72,7 +72,7 @@ def tile_successiveswintransfomerblock_pa_kernel(
         z_pool = stack.enter_context(tc.tile_pool(name="z_pool", bufs=3))
         w_pool = stack.enter_context(tc.tile_pool(name="w_pool", bufs=TENSORS * PASSES))
         wg_pool = stack.enter_context(tc.tile_pool(name="wg_pool", bufs=4))
-        stage_pool = stack.enter_context(tc.tile_pool(name="stage_pool", bufs=4))
+        stage_pool = stack.enter_context(tc.tile_pool(name="stage_pool", bufs=3))
         psum = stack.enter_context(tc.psum_pool(name="psum", bufs=8))
 
         x_rounds = []

@@ -29,12 +29,16 @@ PACK = 4
 PASSES = D // (P * PACK)
 K_BLOCKS = D // P
 N_TILE = 512
-TOKEN_TILES = IMAGES * PATCHES // P
-TILES_PER_ROUND = 3
-ROUNDS = TOKEN_TILES // TILES_PER_ROUND
+HALVES = D // N_TILE
+TILE_PATCHES = P // IMAGES
+TOKEN_TILES = PATCHES // TILE_PATCHES
+ROUND_TILES = WINDOW * SIDE // TILE_PATCHES
+ROUNDS = GRID
 STATS_CHUNK = 512
 
-RUN = 4
+RUN = 2
+
+SCALAR_EVERY = 3
 
 FLOPS = 2 * IMAGES * PATCHES * D * TENSORS * D
 
@@ -50,11 +54,11 @@ def cyclic_pieces(first, count, period):
 
 def window_groups():
     groups = []
-    position = 0
-    while position < POSITIONS:
-        size = RUN if position + RUN <= POSITIONS else 1
-        groups.append((position, size))
-        position += size
+    slot = 0
+    while slot < POSITIONS:
+        size = RUN if slot + RUN <= POSITIONS else 1
+        groups.append((slot, size))
+        slot += size
     return groups
 
 
@@ -63,28 +67,35 @@ def tile_successiveswintransfomerblock_pa_kernel(
 ):
     nc = tc.nc
     outs = [out_0, out_1, out_2]
-    groups = window_groups()
 
     with ExitStack() as stack:
         keep = stack.enter_context(tc.tile_pool(name="keep", bufs=1))
-        x_pool = stack.enter_context(tc.tile_pool(name="x_pool", bufs=ROUNDS))
+        x_pool = stack.enter_context(tc.tile_pool(name="x_pool", bufs=TOKEN_TILES))
         small = stack.enter_context(tc.tile_pool(name="small", bufs=ROUNDS))
-        z_pool = stack.enter_context(tc.tile_pool(name="z_pool", bufs=3))
+        z_pool = stack.enter_context(tc.tile_pool(name="z_pool", bufs=2 * ROUND_TILES))
         w_pool = stack.enter_context(tc.tile_pool(name="w_pool", bufs=TENSORS * PASSES))
         wg_pool = stack.enter_context(tc.tile_pool(name="wg_pool", bufs=4))
-        stage_pool = stack.enter_context(tc.tile_pool(name="stage_pool", bufs=3))
-        psum = stack.enter_context(tc.psum_pool(name="psum", bufs=8))
+        stage_pool = stack.enter_context(tc.tile_pool(name="stage_pool", bufs=4))
+        psum = stack.enter_context(tc.psum_pool(name="psum", bufs=4))
 
-        x_rounds = []
-        for r in range(ROUNDS):
-            x_round = x_pool.tile([P, TILES_PER_ROUND, D], BF16, name="x_round")
+        def load_tokens(a):
+            x_tile = x_pool.tile([P, D], BF16, name="x_tile")
             for b in range(IMAGES):
-                tiles = x_mid[b].rearrange("(a i) k -> i a k", i=P // IMAGES)
-                nc.sync.dma_start(
-                    out=x_round[b:P:IMAGES, :, :],
-                    in_=tiles[:, r * TILES_PER_ROUND : (r + 1) * TILES_PER_ROUND, :],
-                )
-            x_rounds.append(x_round)
+                for offset, start, length in cyclic_pieces(
+                    a * TILE_PATCHES + SHIFT * SIDE, TILE_PATCHES, PATCHES
+                ):
+                    nc.sync.dma_start(
+                        out=x_tile[IMAGES * offset + b : IMAGES * (offset + length) : IMAGES, :],
+                        in_=x_mid[b][start : start + length, :],
+                    )
+            return x_tile
+
+        w_rows = Wqkv2.rearrange("(c t p) n -> c p t n", t=PACK, p=P)
+
+        def load_weights(tensor, c):
+            raw = w_pool.tile([P, PACK, D], BF16, name="w_raw")
+            nc.sync.dma_start(out=raw[:], in_=w_rows[c][:, :, tensor * D : (tensor + 1) * D])
+            return raw
 
         gb_rows = keep.tile([P, P], BF16)
         nc.vector.memset(gb_rows[:], 0.0)
@@ -93,77 +104,88 @@ def tile_successiveswintransfomerblock_pa_kernel(
             out=gb_rows[K_BLOCKS : 2 * K_BLOCKS, :], in_=b3.rearrange("(r c) -> r c", c=P)
         )
 
-        w_rows = Wqkv2.rearrange("(c t p) n -> c p t n", t=PACK, p=P)
+        x_tiles = []
         w_raw = {}
         bias_bc = keep.tile([P, TENSORS * D], BF16)
-        for tensor in range(TENSORS):
+        for r in range(ROUNDS):
+            for a in range(r * ROUND_TILES, (r + 1) * ROUND_TILES):
+                x_tiles.append(load_tokens(a))
+            if r == 0:
+                for c in range(PASSES):
+                    w_raw[(0, c)] = load_weights(0, c)
+        nc.sync.dma_start(out=bias_bc[:], in_=bqkv2.partition_broadcast(P))
+        for tensor in range(1, TENSORS):
             for c in range(PASSES):
-                raw = w_pool.tile([P, PACK, D], BF16, name="w_raw")
-                nc.sync.dma_start(out=raw[:], in_=w_rows[c][:, :, tensor * D : (tensor + 1) * D])
-                w_raw[(tensor, c)] = raw
-            if tensor == 0:
-                nc.sync.dma_start(out=bias_bc[:], in_=bqkv2.partition_broadcast(P))
+                w_raw[(tensor, c)] = load_weights(tensor, c)
 
         ident = keep.tile([P, P], F32)
         make_identity(nc, ident[:])
         gb_rows_f32 = keep.tile([P, P], F32)
         nc.vector.tensor_copy(out=gb_rows_f32[:], in_=gb_rows[:])
-        gb_bank = psum.tile([P, N_TILE], F32, tag="bank")
+        gb_bank = psum.tile([P, N_TILE], F32, tag="flip")
         nc.tensor.transpose(out=gb_bank[:, 0:P], in_=gb_rows_f32[:], identity=ident[:])
         gb_cols = keep.tile([P, 2 * K_BLOCKS], F32)
         nc.vector.tensor_copy(out=gb_cols[:], in_=gb_bank[:, 0 : 2 * K_BLOCKS])
 
         planes = keep.tile([P, K_BLOCKS, IMAGES * PATCHES], BF16)
-        for r in range(ROUNDS):
-            x_round = x_rounds[r]
-            stats = small.tile([P, TILES_PER_ROUND, D // STATS_CHUNK, 6], F32)
-            mean_var = small.tile([P, TILES_PER_ROUND, 2], F32)
-            for a in range(TILES_PER_ROUND):
+
+        mean_var = keep.tile([P, TOKEN_TILES, 2], F32)
+        std = keep.tile([P, TOKEN_TILES], F32)
+        rstd = keep.tile([P, TOKEN_TILES], F32)
+
+        def statistics(r):
+            tiles = slice(r * ROUND_TILES, (r + 1) * ROUND_TILES)
+            stats = small.tile([P, ROUND_TILES, D // STATS_CHUNK, 6], F32, name="stats")
+            for a in range(ROUND_TILES):
+                x_tile = x_tiles[r * ROUND_TILES + a]
                 for h in range(D // STATS_CHUNK):
                     nc.vector.bn_stats(
                         out=stats[:, a, h, :],
-                        in_=x_round[:, a, h * STATS_CHUNK : (h + 1) * STATS_CHUNK],
+                        in_=x_tile[:, h * STATS_CHUNK : (h + 1) * STATS_CHUNK],
                     )
                 nc.vector.bn_aggr(
-                    out=mean_var[:, a, :], in_=stats[:, a, :, :].rearrange("p h s -> p (h s)")
+                    out=mean_var[:, r * ROUND_TILES + a, :],
+                    in_=stats[:, a, :, :].rearrange("p h s -> p (h s)"),
                 )
-            std = small.tile([P, TILES_PER_ROUND], F32)
-            nc.scalar.activation(out=std[:], in_=mean_var[:, :, 1], func=ACT.Sqrt, bias=LN_EPS)
-            rstd = small.tile([P, TILES_PER_ROUND], F32)
-            nc.vector.reciprocal(out=rstd[:], in_=std[:])
-            shift = small.tile([P, TILES_PER_ROUND], F32)
-            nc.vector.scalar_tensor_tensor(
-                out=shift[:], in0=mean_var[:, :, 0], scalar=-1.0, in1=rstd[:],
-                op0=ALU.mult, op1=ALU.mult,
+            nc.scalar.activation(
+                out=std[:, tiles], in_=mean_var[:, tiles, 1], func=ACT.Sqrt, bias=LN_EPS
             )
 
-            banks = [
-                psum.tile([P, N_TILE], F32, name="bank%d" % j, tag="bank") for j in range(K_BLOCKS)
-            ]
-            for a in range(TILES_PER_ROUND):
-                z = z_pool.tile([P, D], F32)
-                nc.scalar.activation(
-                    out=z[:], in_=x_round[:, a, :], func=ACT.Identity,
-                    scale=rstd[:, a : a + 1], bias=shift[:, a : a + 1],
+        z_tiles = {}
+
+        def normalise(r):
+            tiles = slice(r * ROUND_TILES, (r + 1) * ROUND_TILES)
+            nc.vector.reciprocal(out=rstd[:, tiles], in_=std[:, tiles])
+            for a in range(r * ROUND_TILES, (r + 1) * ROUND_TILES):
+                z = z_pool.tile([P, D], F32, name="z")
+                nc.vector.tensor_scalar(
+                    out=z[:], in0=x_tiles[a][:],
+                    scalar1=mean_var[:, a, 0:1], scalar2=rstd[:, a : a + 1],
+                    op0=ALU.subtract, op1=ALU.mult,
                 )
-                for j in range(K_BLOCKS):
+                z_tiles[a] = z
+
+        def flip(r):
+            width = ROUND_TILES * P
+            for j in range(K_BLOCKS):
+                bank = psum.tile([P, N_TILE], F32, name="flipped", tag="flip")
+                for a in range(ROUND_TILES):
                     nc.tensor.transpose(
-                        out=banks[j][:, a * P : (a + 1) * P],
-                        in_=z[:, j * P : (j + 1) * P],
+                        out=bank[:, a * P : (a + 1) * P],
+                        in_=z_tiles[r * ROUND_TILES + a][:, j * P : (j + 1) * P],
                         identity=ident[:],
                     )
-            width = TILES_PER_ROUND * P
-            for j in range(K_BLOCKS):
                 nc.scalar.activation(
-                    out=planes[:, j, r * width : (r + 1) * width], in_=banks[j][:, 0:width],
-                    func=ACT.Identity,
-                    scale=gb_cols[:, j : j + 1], bias=gb_cols[:, K_BLOCKS + j : K_BLOCKS + j + 1],
+                    out=planes[:, j, r * width : (r + 1) * width], in_=bank[:, 0:width],
+                    func=ACT.Identity, scale=gb_cols[:, j : j + 1],
+                    bias=gb_cols[:, K_BLOCKS + j : K_BLOCKS + j + 1],
                 )
 
         x_grouped = keep.tile([P, PASSES, TOKEN_TILES * P, PACK], BF16, align_bytes=64)
         x_codes = keep.tile([P, PASSES, TOKEN_TILES * P], U32, align_bytes=64)
         x_scales = keep.tile([P, PASSES, TOKEN_TILES * P], U8, align_bytes=64)
-        for first, size in groups:
+
+        def gather_windows(first, size):
             for c in range(PASSES):
                 image = planes[:, c * PACK : (c + 1) * PACK, :].rearrange(
                     "p t (r c b) -> p r c b t", r=SIDE, c=SIDE, b=IMAGES
@@ -173,17 +195,14 @@ def tile_successiveswintransfomerblock_pa_kernel(
                         "p (i q x b) t -> p i q x b t", i=WINDOW, x=size, b=IMAGES
                     )
                     for x in range(size):
-                        window_row, window_col = divmod(first + x, GRID)
-                        for i0, r0, rows in cyclic_pieces(window_row * WINDOW - SHIFT, WINDOW, SIDE):
-                            for j0, c0, cols in cyclic_pieces(
-                                window_col * WINDOW - SHIFT, WINDOW, SIDE
-                            ):
-                                nc.vector.tensor_copy(
-                                    out=tile_cols[
-                                        :, i0 : i0 + rows, j0 // size : (j0 + cols) // size, x, :, :
-                                    ],
-                                    in_=image[:, r0 : r0 + rows, c0 + g : c0 + cols : size, :, :],
-                                )
+                        r, window_col = divmod(first + x, GRID)
+                        for j0, c0, cols in cyclic_pieces(window_col * WINDOW - SHIFT, WINDOW, SIDE):
+                            nc.vector.tensor_copy(
+                                out=tile_cols[:, :, j0 // size : (j0 + cols) // size, x, :, :],
+                                in_=image[
+                                    :, r * WINDOW : (r + 1) * WINDOW, c0 + g : c0 + cols : size, :, :
+                                ],
+                            )
             for c in range(PASSES):
                 cols = slice(first * P, (first + size) * P)
                 nc.vector.quantize_mx(
@@ -195,56 +214,100 @@ def tile_successiveswintransfomerblock_pa_kernel(
         w_codes = keep.tile([P, PASSES, TENSORS * D], U32, align_bytes=64)
         w_scales = keep.tile([P, PASSES, TENSORS * D], U8, align_bytes=64)
 
+        w_grouped = {}
+
+        def regroup_weights(tensor, half):
+            for c in range(PASSES):
+                rows = w_raw[(tensor, c)][:, :, half * N_TILE : (half + 1) * N_TILE]
+                grouped = wg_pool.tile([P, N_TILE, PACK], BF16, name="w_grouped", align_bytes=64)
+                copy = nc.vector.tensor_copy if c == 0 else nc.scalar.copy
+                copy(
+                    out=grouped[:].rearrange("p (n i) t -> p n t i", i=4),
+                    in_=rows.rearrange("p t (n i) -> p n t i", i=4),
+                )
+                w_grouped[(half, c)] = grouped
+
         def quantise_weights(tensor):
-            for half in range(D // N_TILE):
+            for half in range(HALVES):
                 for c in range(PASSES):
-                    rows = w_raw[(tensor, c)][:, :, half * N_TILE : (half + 1) * N_TILE]
-                    grouped = wg_pool.tile([P, N_TILE, PACK], BF16, name="w_grouped", align_bytes=64)
-                    nc.scalar.copy(
-                        out=grouped[:].rearrange("p (n i) t -> p n t i", i=4),
-                        in_=rows.rearrange("p t (n i) -> p n t i", i=4),
-                    )
                     cols = slice(tensor * D + half * N_TILE, tensor * D + (half + 1) * N_TILE)
                     nc.vector.quantize_mx(
                         out=w_codes[:, c, cols].bitcast(FP8X4),
                         scales=w_scales[:, c, cols],
-                        in_=grouped[:].rearrange("p n t -> p (n t)"),
+                        in_=w_grouped[(half, c)][:].rearrange("p n t -> p (n t)"),
                     )
 
-        quantise_weights(0)
-        for tensor in range(TENSORS):
-            if tensor + 1 < TENSORS:
-                quantise_weights(tensor + 1)
-            for first, size in groups:
-                stage = stage_pool.tile([P, HEADS, size, HEAD_DIM], F32, name="stage", tag="stage")
-                for g in range(size):
-                    tokens = slice((first + g) * P, (first + g + 1) * P)
-                    for half in range(D // N_TILE):
-                        cols = slice(tensor * D + half * N_TILE, tensor * D + (half + 1) * N_TILE)
-                        acc = psum.tile([P, N_TILE], F32, name="acc", tag="bank")
-                        for c in range(PASSES):
-                            nc.tensor.matmul_mx(
-                                out=acc[:],
-                                lhsT=x_codes[:, c, tokens].bitcast(FP8X4),
-                                lhsT_scale=x_scales[:, c, tokens],
-                                rhs=w_codes[:, c, cols].bitcast(FP8X4),
-                                rhs_scale=w_scales[:, c, cols],
-                                start=(c == 0),
-                                stop=(c == PASSES - 1),
-                            )
-                        heads = slice(half * N_TILE // HEAD_DIM, (half + 1) * N_TILE // HEAD_DIM)
-                        nc.vector.tensor_tensor(
-                            out=stage[:, heads, g, :],
-                            in0=acc[:].rearrange("p (h d) -> p h d", d=HEAD_DIM),
-                            in1=bias_bc[:, cols].rearrange("p (h d) -> p h d", d=HEAD_DIM),
+        def project(tensor, first, size):
+            stage = stage_pool.tile([P, HEADS, size, HEAD_DIM], F32, name="stage", tag="stage")
+            for g in range(size):
+                tokens = slice((first + g) * P, (first + g + 1) * P)
+                for half in range(HALVES):
+                    cols = slice(tensor * D + half * N_TILE, tensor * D + (half + 1) * N_TILE)
+                    acc = psum.tile([P, N_TILE], F32, name="acc", tag="acc")
+                    for c in range(PASSES):
+                        nc.tensor.matmul_mx(
+                            out=acc[:],
+                            lhsT=x_codes[:, c, tokens].bitcast(FP8X4),
+                            lhsT_scale=x_scales[:, c, tokens],
+                            rhs=w_codes[:, c, cols].bitcast(FP8X4),
+                            rhs_scale=w_scales[:, c, cols],
+                            start=(c == 0),
+                            stop=(c == PASSES - 1),
+                        )
+                    heads = slice(half * N_TILE // HEAD_DIM, (half + 1) * N_TILE // HEAD_DIM)
+                    product = acc[:].rearrange("p (h d) -> p h d", d=HEAD_DIM)
+                    bias = bias_bc[:, cols].rearrange("p (h d) -> p h d", d=HEAD_DIM)
+                    if (HALVES * (first + g) + half) % SCALAR_EVERY == SCALAR_EVERY - 1:
+                        nc.scalar.copy(out=stage[:, heads, g, :], in_=product)
+                        nc.gpsimd.tensor_tensor(
+                            out=stage[:, heads, g, :], in0=stage[:, heads, g, :], in1=bias,
                             op=ALU.add,
                         )
-                for x in range(size):
-                    for b in range(IMAGES):
-                        window = b * POSITIONS + first + x
-                        nc.sync.dma_start(
-                            out=outs[tensor][window].rearrange("h (j g) d -> j h (g d)", g=size),
-                            in_=stage[IMAGES * x + b : P : IMAGES * size].rearrange(
-                                "p h g d -> p h (g d)"
-                            ),
+                    else:
+                        nc.vector.tensor_tensor(
+                            out=stage[:, heads, g, :], in0=product, in1=bias, op=ALU.add
                         )
+            for x in range(size):
+                r, window_col = divmod(first + x, GRID)
+                window_row = (r + 1) % GRID
+                for b in range(IMAGES):
+                    window = b * POSITIONS + window_row * GRID + window_col
+                    nc.sync.dma_start(
+                        out=outs[tensor][window].rearrange("h (j g) d -> j h (g d)", g=size),
+                        in_=stage[IMAGES * x + b : P : IMAGES * size].rearrange(
+                            "p h g d -> p h (g d)"
+                        ),
+                    )
+
+        groups = window_groups()
+
+        def project_and_prepare(tensor, index):
+            project(tensor, *groups[index])
+            if tensor + 1 < TENSORS and index < HALVES:
+                regroup_weights(tensor + 1, index)
+
+        statistics(0)
+        normalise(0)
+        flip(0)
+        for r in range(ROUNDS):
+            complete = [
+                i for i in range(len(groups)) if r * GRID < sum(groups[i]) <= (r + 1) * GRID
+            ]
+            if r + 1 < ROUNDS:
+                statistics(r + 1)
+            if r == 0:
+                for half in range(HALVES):
+                    regroup_weights(0, half)
+            if r + 1 < ROUNDS:
+                normalise(r + 1)
+                flip(r + 1)
+            for i in complete:
+                gather_windows(*groups[i])
+            if r == 0:
+                quantise_weights(0)
+            for i in complete:
+                project_and_prepare(0, i)
+        for tensor in range(1, TENSORS):
+            quantise_weights(tensor)
+            for i in range(len(groups)):
+                project_and_prepare(tensor, i)

@@ -14,7 +14,6 @@ ALU = mybir.AluOpType
 P = 128
 IMAGES = 2
 SIDE = 24
-PATCHES = SIDE * SIDE
 WINDOW = 8
 SHIFT = 4
 GRID = SIDE // WINDOW
@@ -30,17 +29,20 @@ PASSES = D // (P * PACK)
 K_BLOCKS = D // P
 N_TILE = 512
 HALVES = D // N_TILE
-TILE_PATCHES = P // IMAGES
-TOKEN_TILES = PATCHES // TILE_PATCHES
-ROUND_TILES = WINDOW * SIDE // TILE_PATCHES
-ROUNDS = GRID
+BANK_HEADS = N_TILE // HEAD_DIM
+TOKEN_TILES = IMAGES * SIDE * SIDE // P
+ROUND_TILES = 3
+ROUNDS = TOKEN_TILES // ROUND_TILES
 STATS_CHUNK = 512
 
-RUN = 2
+MAIN_WINDOWS = P // WINDOW
+LAST_WINDOWS = IMAGES * POSITIONS - MAIN_WINDOWS
+LAST_ROWS = (SIDE + 2 * WINDOW - SHIFT, SIDE + 3 * WINDOW - SHIFT)
+EDGE_BASE = P - IMAGES * SIDE
 
 SCALAR_EVERY = 3
 
-FLOPS = 2 * IMAGES * PATCHES * D * TENSORS * D
+FLOPS = 2 * IMAGES * SIDE * SIDE * D * TENSORS * D
 
 
 def cyclic_pieces(first, count, period):
@@ -52,14 +54,9 @@ def cyclic_pieces(first, count, period):
     return pieces
 
 
-def window_groups():
-    groups = []
-    slot = 0
-    while slot < POSITIONS:
-        size = RUN if slot + RUN <= POSITIONS else 1
-        groups.append((slot, size))
-        slot += size
-    return groups
+def inner_partition(row):
+    skipped = LAST_ROWS[1] - LAST_ROWS[0] if row >= LAST_ROWS[1] else 0
+    return 2 * (row - skipped)
 
 
 def tile_successiveswintransfomerblock_pa_kernel(
@@ -70,32 +67,45 @@ def tile_successiveswintransfomerblock_pa_kernel(
 
     with ExitStack() as stack:
         keep = stack.enter_context(tc.tile_pool(name="keep", bufs=1))
-        x_pool = stack.enter_context(tc.tile_pool(name="x_pool", bufs=TOKEN_TILES))
         small = stack.enter_context(tc.tile_pool(name="small", bufs=ROUNDS))
         z_pool = stack.enter_context(tc.tile_pool(name="z_pool", bufs=2 * ROUND_TILES))
-        w_pool = stack.enter_context(tc.tile_pool(name="w_pool", bufs=TENSORS * PASSES))
+        round_pool = stack.enter_context(tc.tile_pool(name="round_pool", bufs=2))
+        w_pool = stack.enter_context(tc.tile_pool(name="w_pool", bufs=2 * PASSES))
         wg_pool = stack.enter_context(tc.tile_pool(name="wg_pool", bufs=4))
-        stage_pool = stack.enter_context(tc.tile_pool(name="stage_pool", bufs=4))
+        stage_pool = stack.enter_context(tc.tile_pool(name="stage_pool", bufs=3))
+        last_pool = stack.enter_context(tc.tile_pool(name="last_pool", bufs=2))
         psum = stack.enter_context(tc.psum_pool(name="psum", bufs=4))
 
-        def load_tokens(a):
-            x_tile = x_pool.tile([P, D], BF16, name="x_tile")
-            for b in range(IMAGES):
-                for offset, start, length in cyclic_pieces(
-                    a * TILE_PATCHES + SHIFT * SIDE, TILE_PATCHES, PATCHES
-                ):
-                    nc.sync.dma_start(
-                        out=x_tile[IMAGES * offset + b : IMAGES * (offset + length) : IMAGES, :],
-                        in_=x_mid[b][start : start + length, :],
-                    )
-            return x_tile
+        x_rows = x_mid.rearrange("b (r c) k -> (b r) c k", c=SIDE)
+        x_main = keep.tile([P, WINDOW, D], BF16)
+        x_last = keep.tile([P, D], BF16)
+
+        def load_columns(j0, j1):
+            for row0, row1 in ((0, LAST_ROWS[0]), (LAST_ROWS[1], IMAGES * SIDE)):
+                inner = x_rows[row0:row1, SHIFT : SHIFT + 2 * WINDOW, :].rearrange(
+                    "r (w j) k -> r w j k", w=2
+                )
+                nc.sync.dma_start(
+                    out=x_main[inner_partition(row0) : inner_partition(row1 - 1) + 2, j0:j1, :]
+                    .rearrange("p j k -> p (j k)"),
+                    in_=inner[:, :, j0:j1, :].rearrange("r w j k -> r w (j k)"),
+                )
+            for offset, c0, cols in cyclic_pieces(j0 - SHIFT, j1 - j0, SIDE):
+                nc.sync.dma_start(
+                    out=x_main[EDGE_BASE:P, j0 + offset : j0 + offset + cols, :].rearrange(
+                        "p j k -> p (j k)"
+                    ),
+                    in_=x_rows[:, c0 : c0 + cols, :].rearrange("r c k -> r (c k)"),
+                )
 
         w_rows = Wqkv2.rearrange("(c t p) n -> c p t n", t=PACK, p=P)
+        w_raw = {}
 
-        def load_weights(tensor, c):
-            raw = w_pool.tile([P, PACK, D], BF16, name="w_raw")
-            nc.sync.dma_start(out=raw[:], in_=w_rows[c][:, :, tensor * D : (tensor + 1) * D])
-            return raw
+        def load_weights(tensor):
+            for c in range(PASSES):
+                raw = w_pool.tile([P, PACK, D], BF16, name="w_raw")
+                nc.sync.dma_start(out=raw[:], in_=w_rows[c][:, :, tensor * D : (tensor + 1) * D])
+                w_raw[(tensor, c)] = raw
 
         gb_rows = keep.tile([P, P], BF16)
         nc.vector.memset(gb_rows[:], 0.0)
@@ -104,19 +114,18 @@ def tile_successiveswintransfomerblock_pa_kernel(
             out=gb_rows[K_BLOCKS : 2 * K_BLOCKS, :], in_=b3.rearrange("(r c) -> r c", c=P)
         )
 
-        x_tiles = []
-        w_raw = {}
+        nc.sync.dma_start(
+            out=x_last[:], in_=x_rows[LAST_ROWS[0] : LAST_ROWS[1], SHIFT : SHIFT + 2 * WINDOW, :]
+        )
+        load_columns(0, ROUND_TILES - 1)
+        load_weights(0)
+        for r in range(1, ROUNDS):
+            load_columns(r * ROUND_TILES - 1, (r + 1) * ROUND_TILES - 1)
         bias_bc = keep.tile([P, TENSORS * D], BF16)
-        for r in range(ROUNDS):
-            for a in range(r * ROUND_TILES, (r + 1) * ROUND_TILES):
-                x_tiles.append(load_tokens(a))
-            if r == 0:
-                for c in range(PASSES):
-                    w_raw[(0, c)] = load_weights(0, c)
         nc.sync.dma_start(out=bias_bc[:], in_=bqkv2.partition_broadcast(P))
         for tensor in range(1, TENSORS):
-            for c in range(PASSES):
-                w_raw[(tensor, c)] = load_weights(tensor, c)
+            load_weights(tensor)
+        x_tiles = [x_last[:]] + [x_main[:, j, :] for j in range(WINDOW)]
 
         ident = keep.tile([P, P], F32)
         make_identity(nc, ident[:])
@@ -127,21 +136,45 @@ def tile_successiveswintransfomerblock_pa_kernel(
         gb_cols = keep.tile([P, 2 * K_BLOCKS], F32)
         nc.vector.tensor_copy(out=gb_cols[:], in_=gb_bank[:, 0 : 2 * K_BLOCKS])
 
-        planes = keep.tile([P, K_BLOCKS, IMAGES * PATCHES], BF16)
+        sort_main = keep.tile([P, P], F32)
+        for b in range(IMAGES):
+            for window_row in range(GRID):
+                window = b * POSITIONS + window_row * GRID
+                for i0, r0, rows in cyclic_pieces(window_row * WINDOW - SHIFT, WINDOW, SIDE):
+                    row = b * SIDE + r0
+                    nc.vector.tensor_copy(
+                        out=sort_main[:, window * WINDOW + i0 : window * WINDOW + i0 + rows],
+                        in_=ident[:, EDGE_BASE + row : EDGE_BASE + row + rows],
+                    )
+                    if window + 2 < MAIN_WINDOWS:
+                        first = inner_partition(row)
+                        nc.vector.tensor_copy(
+                            out=sort_main[:, (window + 1) * WINDOW : (window + 3) * WINDOW]
+                            .rearrange("p (w i) -> p w i", w=2)[:, :, i0 : i0 + rows],
+                            in_=ident[:, first : first + 2 * rows].rearrange("p (i w) -> p w i", w=2),
+                        )
+        sort_last = keep.tile([P, P], F32)
+        nc.vector.tensor_copy(
+            out=sort_last[:].rearrange("p (i j w) -> p i j w", i=WINDOW, w=LAST_WINDOWS),
+            in_=ident[:].rearrange("p (i w j) -> p i j w", i=WINDOW, w=LAST_WINDOWS),
+        )
+        sorts = [sort_last] + [sort_main] * WINDOW
 
         mean_var = keep.tile([P, TOKEN_TILES, 2], F32)
         std = keep.tile([P, TOKEN_TILES], F32)
         rstd = keep.tile([P, TOKEN_TILES], F32)
+        x_codes = keep.tile([P, PASSES, TOKEN_TILES * P], U32, align_bytes=64)
+        x_scales = keep.tile([P, PASSES, TOKEN_TILES * P], U8, align_bytes=64)
+        width = ROUND_TILES * P
 
-        def statistics(r):
+        def layer_norm(r):
             tiles = slice(r * ROUND_TILES, (r + 1) * ROUND_TILES)
             stats = small.tile([P, ROUND_TILES, D // STATS_CHUNK, 6], F32, name="stats")
             for a in range(ROUND_TILES):
-                x_tile = x_tiles[r * ROUND_TILES + a]
                 for h in range(D // STATS_CHUNK):
                     nc.vector.bn_stats(
                         out=stats[:, a, h, :],
-                        in_=x_tile[:, h * STATS_CHUNK : (h + 1) * STATS_CHUNK],
+                        in_=x_tiles[r * ROUND_TILES + a][:, h * STATS_CHUNK : (h + 1) * STATS_CHUNK],
                     )
                 nc.vector.bn_aggr(
                     out=mean_var[:, r * ROUND_TILES + a, :],
@@ -150,164 +183,119 @@ def tile_successiveswintransfomerblock_pa_kernel(
             nc.scalar.activation(
                 out=std[:, tiles], in_=mean_var[:, tiles, 1], func=ACT.Sqrt, bias=LN_EPS
             )
-
-        z_tiles = {}
-
-        def normalise(r):
-            tiles = slice(r * ROUND_TILES, (r + 1) * ROUND_TILES)
             nc.vector.reciprocal(out=rstd[:, tiles], in_=std[:, tiles])
+            z_tiles = []
             for a in range(r * ROUND_TILES, (r + 1) * ROUND_TILES):
                 z = z_pool.tile([P, D], F32, name="z")
                 nc.vector.tensor_scalar(
-                    out=z[:], in0=x_tiles[a][:],
+                    out=z[:], in0=x_tiles[a],
                     scalar1=mean_var[:, a, 0:1], scalar2=rstd[:, a : a + 1],
                     op0=ALU.subtract, op1=ALU.mult,
                 )
-                z_tiles[a] = z
-
-        def flip(r):
-            width = ROUND_TILES * P
+                z_tiles.append(z)
+            planes = round_pool.tile([P, K_BLOCKS, width], BF16, name="planes")
             for j in range(K_BLOCKS):
                 bank = psum.tile([P, N_TILE], F32, name="flipped", tag="flip")
                 for a in range(ROUND_TILES):
                     nc.tensor.transpose(
                         out=bank[:, a * P : (a + 1) * P],
-                        in_=z_tiles[r * ROUND_TILES + a][:, j * P : (j + 1) * P],
-                        identity=ident[:],
+                        in_=z_tiles[a][:, j * P : (j + 1) * P],
+                        identity=sorts[r * ROUND_TILES + a][:],
                     )
                 nc.scalar.activation(
-                    out=planes[:, j, r * width : (r + 1) * width], in_=bank[:, 0:width],
+                    out=planes[:, j, :], in_=bank[:, 0:width],
                     func=ACT.Identity, scale=gb_cols[:, j : j + 1],
                     bias=gb_cols[:, K_BLOCKS + j : K_BLOCKS + j + 1],
                 )
-
-        x_grouped = keep.tile([P, PASSES, TOKEN_TILES * P, PACK], BF16, align_bytes=64)
-        x_codes = keep.tile([P, PASSES, TOKEN_TILES * P], U32, align_bytes=64)
-        x_scales = keep.tile([P, PASSES, TOKEN_TILES * P], U8, align_bytes=64)
-
-        def gather_windows(first, size):
+            grouped = round_pool.tile([P, PASSES, width, PACK], BF16, name="x_grouped", align_bytes=64)
             for c in range(PASSES):
-                image = planes[:, c * PACK : (c + 1) * PACK, :].rearrange(
-                    "p t (r c b) -> p r c b t", r=SIDE, c=SIDE, b=IMAGES
+                nc.vector.tensor_copy(
+                    out=grouped[:, c, :, :].rearrange("p (n i) t -> p n t i", i=4),
+                    in_=planes[:, c * PACK : (c + 1) * PACK, :].rearrange("p t (n i) -> p n t i", i=4),
                 )
-                for g in range(size):
-                    tile_cols = x_grouped[:, c, (first + g) * P : (first + g + 1) * P, :].rearrange(
-                        "p (i q x b) t -> p i q x b t", i=WINDOW, x=size, b=IMAGES
+            for c in range(PASSES):
+                for a in range(ROUND_TILES):
+                    cols = slice((r * ROUND_TILES + a) * P, (r * ROUND_TILES + a + 1) * P)
+                    nc.vector.quantize_mx(
+                        out=x_codes[:, c, cols].bitcast(FP8X4),
+                        scales=x_scales[:, c, cols],
+                        in_=grouped[:, c, a * P : (a + 1) * P, :].rearrange("p m t -> p (m t)"),
                     )
-                    for x in range(size):
-                        r, window_col = divmod(first + x, GRID)
-                        for j0, c0, cols in cyclic_pieces(window_col * WINDOW - SHIFT, WINDOW, SIDE):
-                            nc.vector.tensor_copy(
-                                out=tile_cols[:, :, j0 // size : (j0 + cols) // size, x, :, :],
-                                in_=image[
-                                    :, r * WINDOW : (r + 1) * WINDOW, c0 + g : c0 + cols : size, :, :
-                                ],
-                            )
-            for c in range(PASSES):
-                cols = slice(first * P, (first + size) * P)
-                nc.vector.quantize_mx(
-                    out=x_codes[:, c, cols].bitcast(FP8X4),
-                    scales=x_scales[:, c, cols],
-                    in_=x_grouped[:, c, cols, :].rearrange("p m t -> p (m t)"),
-                )
 
         w_codes = keep.tile([P, PASSES, TENSORS * D], U32, align_bytes=64)
         w_scales = keep.tile([P, PASSES, TENSORS * D], U8, align_bytes=64)
 
-        w_grouped = {}
-
-        def regroup_weights(tensor, half):
-            for c in range(PASSES):
-                rows = w_raw[(tensor, c)][:, :, half * N_TILE : (half + 1) * N_TILE]
-                grouped = wg_pool.tile([P, N_TILE, PACK], BF16, name="w_grouped", align_bytes=64)
-                copy = nc.vector.tensor_copy if c == 0 else nc.scalar.copy
-                copy(
-                    out=grouped[:].rearrange("p (n i) t -> p n t i", i=4),
-                    in_=rows.rearrange("p t (n i) -> p n t i", i=4),
-                )
-                w_grouped[(half, c)] = grouped
-
         def quantise_weights(tensor):
             for half in range(HALVES):
                 for c in range(PASSES):
+                    rows = w_raw[(tensor, c)][:, :, half * N_TILE : (half + 1) * N_TILE]
+                    grouped = wg_pool.tile([P, N_TILE, PACK], BF16, name="w_grouped", align_bytes=64)
+                    nc.scalar.copy(
+                        out=grouped[:].rearrange("p (n i) t -> p n t i", i=4),
+                        in_=rows.rearrange("p t (n i) -> p n t i", i=4),
+                    )
                     cols = slice(tensor * D + half * N_TILE, tensor * D + (half + 1) * N_TILE)
                     nc.vector.quantize_mx(
                         out=w_codes[:, c, cols].bitcast(FP8X4),
                         scales=w_scales[:, c, cols],
-                        in_=w_grouped[(half, c)][:].rearrange("p n t -> p (n t)"),
+                        in_=grouped[:].rearrange("p n t -> p (n t)"),
                     )
 
-        def project(tensor, first, size):
-            stage = stage_pool.tile([P, HEADS, size, HEAD_DIM], F32, name="stage", tag="stage")
-            for g in range(size):
-                tokens = slice((first + g) * P, (first + g + 1) * P)
-                for half in range(HALVES):
-                    cols = slice(tensor * D + half * N_TILE, tensor * D + (half + 1) * N_TILE)
-                    acc = psum.tile([P, N_TILE], F32, name="acc", tag="acc")
-                    for c in range(PASSES):
-                        nc.tensor.matmul_mx(
-                            out=acc[:],
-                            lhsT=x_codes[:, c, tokens].bitcast(FP8X4),
-                            lhsT_scale=x_scales[:, c, tokens],
-                            rhs=w_codes[:, c, cols].bitcast(FP8X4),
-                            rhs_scale=w_scales[:, c, cols],
-                            start=(c == 0),
-                            stop=(c == PASSES - 1),
-                        )
-                    heads = slice(half * N_TILE // HEAD_DIM, (half + 1) * N_TILE // HEAD_DIM)
-                    product = acc[:].rearrange("p (h d) -> p h d", d=HEAD_DIM)
-                    bias = bias_bc[:, cols].rearrange("p (h d) -> p h d", d=HEAD_DIM)
-                    if (HALVES * (first + g) + half) % SCALAR_EVERY == SCALAR_EVERY - 1:
-                        nc.scalar.copy(out=stage[:, heads, g, :], in_=product)
-                        nc.gpsimd.tensor_tensor(
-                            out=stage[:, heads, g, :], in0=stage[:, heads, g, :], in1=bias,
-                            op=ALU.add,
-                        )
-                    else:
-                        nc.vector.tensor_tensor(
-                            out=stage[:, heads, g, :], in0=product, in1=bias, op=ALU.add
-                        )
-            for x in range(size):
-                r, window_col = divmod(first + x, GRID)
-                window_row = (r + 1) % GRID
-                for b in range(IMAGES):
-                    window = b * POSITIONS + window_row * GRID + window_col
-                    nc.sync.dma_start(
-                        out=outs[tensor][window].rearrange("h (j g) d -> j h (g d)", g=size),
-                        in_=stage[IMAGES * x + b : P : IMAGES * size].rearrange(
-                            "p h g d -> p h (g d)"
-                        ),
-                    )
+        def project(a, tensor, half, target, by_scalar):
+            tokens = slice(a * P, (a + 1) * P)
+            cols = slice(tensor * D + half * N_TILE, tensor * D + (half + 1) * N_TILE)
+            acc = psum.tile([P, N_TILE], F32, name="acc", tag="acc")
+            for c in range(PASSES):
+                nc.tensor.matmul_mx(
+                    out=acc[:],
+                    lhsT=x_codes[:, c, tokens].bitcast(FP8X4),
+                    lhsT_scale=x_scales[:, c, tokens],
+                    rhs=w_codes[:, c, cols].bitcast(FP8X4),
+                    rhs_scale=w_scales[:, c, cols],
+                    start=(c == 0),
+                    stop=(c == PASSES - 1),
+                )
+            product = acc[:].rearrange("p (h d) -> p h d", d=HEAD_DIM)
+            bias = bias_bc[:, cols].rearrange("p (h d) -> p h d", d=HEAD_DIM)
+            if by_scalar:
+                nc.scalar.copy(out=target, in_=product)
+                nc.gpsimd.tensor_tensor(out=target, in0=target, in1=bias, op=ALU.add)
+            else:
+                nc.vector.tensor_tensor(out=target, in0=product, in1=bias, op=ALU.add)
 
-        groups = window_groups()
+        def project_last(tensor):
+            stage = last_pool.tile([P, HEADS, HEAD_DIM], F32, name="stage_last")
+            for half in range(HALVES):
+                heads = slice(half * BANK_HEADS, (half + 1) * BANK_HEADS)
+                project(0, tensor, half, stage[:, heads, :], False)
+            for w in range(LAST_WINDOWS):
+                nc.sync.dma_start(
+                    out=outs[tensor][MAIN_WINDOWS + w].rearrange("h n d -> n h d"),
+                    in_=stage[w:P:LAST_WINDOWS],
+                )
 
-        def project_and_prepare(tensor, index):
-            project(tensor, *groups[index])
-            if tensor + 1 < TENSORS and index < HALVES:
-                regroup_weights(tensor + 1, index)
+        def project_main(tensor, half):
+            stage = stage_pool.tile([P, BANK_HEADS, WINDOW, HEAD_DIM], F32, name="stage")
+            for j in range(WINDOW):
+                project(
+                    1 + j, tensor, half, stage[:, :, j, :], j % SCALAR_EVERY == SCALAR_EVERY - 1
+                )
+            for h in range(BANK_HEADS):
+                nc.sync.dma_start(
+                    out=outs[tensor][0:MAIN_WINDOWS, half * BANK_HEADS + h, :, :].rearrange(
+                        "w (i j) d -> w i (j d)", j=WINDOW
+                    ),
+                    in_=stage[:, h, :, :].rearrange("p j d -> p (j d)"),
+                )
 
-        statistics(0)
-        normalise(0)
-        flip(0)
-        for r in range(ROUNDS):
-            complete = [
-                i for i in range(len(groups)) if r * GRID < sum(groups[i]) <= (r + 1) * GRID
-            ]
-            if r + 1 < ROUNDS:
-                statistics(r + 1)
-            if r == 0:
-                for half in range(HALVES):
-                    regroup_weights(0, half)
-            if r + 1 < ROUNDS:
-                normalise(r + 1)
-                flip(r + 1)
-            for i in complete:
-                gather_windows(*groups[i])
-            if r == 0:
-                quantise_weights(0)
-            for i in complete:
-                project_and_prepare(0, i)
-        for tensor in range(1, TENSORS):
-            quantise_weights(tensor)
-            for i in range(len(groups)):
-                project_and_prepare(tensor, i)
+        layer_norm(0)
+        quantise_weights(0)
+        project_last(0)
+        for r in range(1, ROUNDS):
+            layer_norm(r)
+        for tensor in range(TENSORS):
+            if tensor + 1 < TENSORS:
+                quantise_weights(tensor + 1)
+                project_last(tensor + 1)
+            for half in range(HALVES):
+                project_main(tensor, half)

@@ -118,13 +118,13 @@ def tile_successiveswintransfomerblock_pa_kernel(
             out=x_last[:], in_=x_rows[LAST_ROWS[0] : LAST_ROWS[1], SHIFT : SHIFT + 2 * WINDOW, :]
         )
         load_columns(0, ROUND_TILES - 1)
-        load_weights(0)
         for r in range(1, ROUNDS):
             load_columns(r * ROUND_TILES - 1, (r + 1) * ROUND_TILES - 1)
+        load_weights(0)
+        load_weights(1)
         bias_bc = keep.tile([P, TENSORS * D], BF16)
         nc.sync.dma_start(out=bias_bc[:], in_=bqkv2.partition_broadcast(P))
-        for tensor in range(1, TENSORS):
-            load_weights(tensor)
+        load_weights(2)
         x_tiles = [x_last[:]] + [x_main[:, j, :] for j in range(WINDOW)]
 
         ident = keep.tile([P, P], F32)
@@ -230,7 +230,8 @@ def tile_successiveswintransfomerblock_pa_kernel(
                 for c in range(PASSES):
                     rows = w_raw[(tensor, c)][:, :, half * N_TILE : (half + 1) * N_TILE]
                     grouped = wg_pool.tile([P, N_TILE, PACK], BF16, name="w_grouped", align_bytes=64)
-                    nc.scalar.copy(
+                    copy = nc.vector.tensor_copy if tensor == 0 and c == 0 else nc.scalar.copy
+                    copy(
                         out=grouped[:].rearrange("p (n i) t -> p n t i", i=4),
                         in_=rows.rearrange("p t (n i) -> p n t i", i=4),
                     )
@@ -288,14 +289,12 @@ def tile_successiveswintransfomerblock_pa_kernel(
                     in_=stage[:, h, :, :].rearrange("p j d -> p (j d)"),
                 )
 
-        layer_norm(0)
-        quantise_weights(0)
-        project_last(0)
-        for r in range(1, ROUNDS):
+        for r in range(ROUNDS):
             layer_norm(r)
+        quantise_weights(0)
         for tensor in range(TENSORS):
-            if tensor + 1 < TENSORS:
-                quantise_weights(tensor + 1)
-                project_last(tensor + 1)
+            project_last(tensor)
             for half in range(HALVES):
                 project_main(tensor, half)
+            if tensor + 1 < TENSORS:
+                quantise_weights(tensor + 1)

@@ -40,7 +40,7 @@ LAST_WINDOWS = IMAGES * POSITIONS - MAIN_WINDOWS
 LAST_ROWS = (SIDE + 2 * WINDOW - SHIFT, SIDE + 3 * WINDOW - SHIFT)
 EDGE_BASE = P - IMAGES * SIDE
 
-SCALAR_EVERY = 3
+SCALAR_EVERY = 2
 
 FLOPS = 2 * IMAGES * SIDE * SIDE * D * TENSORS * D
 

@@ -40,7 +40,7 @@ LAST_WINDOWS = IMAGES * POSITIONS - MAIN_WINDOWS
 LAST_ROWS = (SIDE + 2 * WINDOW - SHIFT, SIDE + 3 * WINDOW - SHIFT)
 EDGE_BASE = P - IMAGES * SIDE
 
-SCALAR_EVERY = 2
+SCALAR_EVERY = 3
 
 FLOPS = 2 * IMAGES * SIDE * SIDE * D * TENSORS * D
 
@@ -163,6 +163,7 @@ def tile_successiveswintransfomerblock_pa_kernel(
         mean_var = keep.tile([P, TOKEN_TILES, 2], F32)
         std = keep.tile([P, TOKEN_TILES], F32)
         rstd = keep.tile([P, TOKEN_TILES], F32)
+        shift = keep.tile([P, TOKEN_TILES], F32)
         x_codes = keep.tile([P, PASSES, TOKEN_TILES * P], U32, align_bytes=64)
         x_scales = keep.tile([P, PASSES, TOKEN_TILES * P], U8, align_bytes=64)
         width = ROUND_TILES * P
@@ -184,13 +185,17 @@ def tile_successiveswintransfomerblock_pa_kernel(
                 out=std[:, tiles], in_=mean_var[:, tiles, 1], func=ACT.Sqrt, bias=LN_EPS
             )
             nc.vector.reciprocal(out=rstd[:, tiles], in_=std[:, tiles])
+            nc.vector.scalar_tensor_tensor(
+                out=shift[:, tiles], in0=mean_var[:, tiles, 0], scalar=-1.0, in1=rstd[:, tiles],
+                op0=ALU.mult, op1=ALU.mult,
+            )
             z_tiles = []
             for a in range(r * ROUND_TILES, (r + 1) * ROUND_TILES):
                 z = z_pool.tile([P, D], F32, name="z")
-                nc.vector.tensor_scalar(
+                nc.gpsimd.tensor_scalar(
                     out=z[:], in0=x_tiles[a],
-                    scalar1=mean_var[:, a, 0:1], scalar2=rstd[:, a : a + 1],
-                    op0=ALU.subtract, op1=ALU.mult,
+                    scalar1=rstd[:, a : a + 1], scalar2=shift[:, a : a + 1],
+                    op0=ALU.mult, op1=ALU.add,
                 )
                 z_tiles.append(z)
             planes = round_pool.tile([P, K_BLOCKS, width], BF16, name="planes")

@@ -163,12 +163,11 @@ def tile_successiveswintransfomerblock_pa_kernel(
         mean_var = keep.tile([P, TOKEN_TILES, 2], F32)
         std = keep.tile([P, TOKEN_TILES], F32)
         rstd = keep.tile([P, TOKEN_TILES], F32)
-        shift = keep.tile([P, TOKEN_TILES], F32)
         x_codes = keep.tile([P, PASSES, TOKEN_TILES * P], U32, align_bytes=64)
         x_scales = keep.tile([P, PASSES, TOKEN_TILES * P], U8, align_bytes=64)
         width = ROUND_TILES * P
 
-        def layer_norm(r):
+        def statistics(r):
             tiles = slice(r * ROUND_TILES, (r + 1) * ROUND_TILES)
             stats = small.tile([P, ROUND_TILES, D // STATS_CHUNK, 6], F32, name="stats")
             for a in range(ROUND_TILES):
@@ -185,17 +184,15 @@ def tile_successiveswintransfomerblock_pa_kernel(
                 out=std[:, tiles], in_=mean_var[:, tiles, 1], func=ACT.Sqrt, bias=LN_EPS
             )
             nc.vector.reciprocal(out=rstd[:, tiles], in_=std[:, tiles])
-            nc.vector.scalar_tensor_tensor(
-                out=shift[:, tiles], in0=mean_var[:, tiles, 0], scalar=-1.0, in1=rstd[:, tiles],
-                op0=ALU.mult, op1=ALU.mult,
-            )
+
+        def normalise(r):
             z_tiles = []
             for a in range(r * ROUND_TILES, (r + 1) * ROUND_TILES):
                 z = z_pool.tile([P, D], F32, name="z")
-                nc.gpsimd.tensor_scalar(
+                nc.vector.tensor_scalar(
                     out=z[:], in0=x_tiles[a],
-                    scalar1=rstd[:, a : a + 1], scalar2=shift[:, a : a + 1],
-                    op0=ALU.mult, op1=ALU.add,
+                    scalar1=mean_var[:, a, 0:1], scalar2=rstd[:, a : a + 1],
+                    op0=ALU.subtract, op1=ALU.mult,
                 )
                 z_tiles.append(z)
             planes = round_pool.tile([P, K_BLOCKS, width], BF16, name="planes")
@@ -295,7 +292,9 @@ def tile_successiveswintransfomerblock_pa_kernel(
                 )
 
         for r in range(ROUNDS):
-            layer_norm(r)
+            statistics(r)
+        for r in range(ROUNDS):
+            normalise(r)
         quantise_weights(0)
         for tensor in range(TENSORS):
             project_last(tensor)

@@ -38,25 +38,21 @@ STATS_CHUNK = 512
 MAIN_WINDOWS = P // WINDOW
 LAST_WINDOWS = IMAGES * POSITIONS - MAIN_WINDOWS
 LAST_ROWS = (SIDE + 2 * WINDOW - SHIFT, SIDE + 3 * WINDOW - SHIFT)
-EDGE_BASE = P - IMAGES * SIDE
+FULL_ROWS = 32
+RUN = 4
 
 SCALAR_EVERY = 3
 
 FLOPS = 2 * IMAGES * SIDE * SIDE * D * TENSORS * D
 
 
-def cyclic_pieces(first, count, period):
-    start = first % period
-    head = min(count, period - start)
-    pieces = [(0, start, head)]
-    if head < count:
-        pieces.append((head, 0, count - head))
-    return pieces
-
-
-def inner_partition(row):
-    skipped = LAST_ROWS[1] - LAST_ROWS[0] if row >= LAST_ROWS[1] else 0
-    return 2 * (row - skipped)
+def home(row, column):
+    if row < FULL_ROWS:
+        return 4 * row + column
+    if column == 0:
+        return 4 * (row - FULL_ROWS) + 3
+    run_start = 16 + 2 * (row - FULL_ROWS) if row < LAST_ROWS[0] else 24 + 2 * (row - LAST_ROWS[1])
+    return 4 * (run_start + column - 1) + 3
 
 
 def tile_successiveswintransfomerblock_pa_kernel(
@@ -81,21 +77,23 @@ def tile_successiveswintransfomerblock_pa_kernel(
         x_last = keep.tile([P, D], BF16)
 
         def load_columns(j0, j1):
-            for row0, row1 in ((0, LAST_ROWS[0]), (LAST_ROWS[1], IMAGES * SIDE)):
-                inner = x_rows[row0:row1, SHIFT : SHIFT + 2 * WINDOW, :].rearrange(
+            groups = [(0, FULL_ROWS, column) for column in range(GRID)]
+            groups.append((FULL_ROWS, IMAGES * SIDE, 0))
+            for row0, row1, column in groups:
+                c0 = (column * WINDOW + j0 - SHIFT) % SIDE
+                nc.sync.dma_start(
+                    out=x_main[home(row0, column) : home(row1 - 1, column) + 1 : 4, j0:j1, :]
+                    .rearrange("p j k -> p (j k)"),
+                    in_=x_rows[row0:row1, c0 : c0 + j1 - j0, :].rearrange("r c k -> r (c k)"),
+                )
+            for row0 in (LAST_ROWS[0] - RUN, LAST_ROWS[1]):
+                inner = x_rows[row0 : row0 + RUN, SHIFT : SHIFT + 2 * WINDOW, :].rearrange(
                     "r (w j) k -> r w j k", w=2
                 )
                 nc.sync.dma_start(
-                    out=x_main[inner_partition(row0) : inner_partition(row1 - 1) + 2, j0:j1, :]
+                    out=x_main[home(row0, 1) : home(row0 + RUN - 1, 2) + 1 : 4, j0:j1, :]
                     .rearrange("p j k -> p (j k)"),
                     in_=inner[:, :, j0:j1, :].rearrange("r w j k -> r w (j k)"),
-                )
-            for offset, c0, cols in cyclic_pieces(j0 - SHIFT, j1 - j0, SIDE):
-                nc.sync.dma_start(
-                    out=x_main[EDGE_BASE:P, j0 + offset : j0 + offset + cols, :].rearrange(
-                        "p j k -> p (j k)"
-                    ),
-                    in_=x_rows[:, c0 : c0 + cols, :].rearrange("r c k -> r (c k)"),
                 )
 
         w_rows = Wqkv2.rearrange("(c t p) n -> c p t n", t=PACK, p=P)
@@ -117,9 +115,8 @@ def tile_successiveswintransfomerblock_pa_kernel(
         nc.sync.dma_start(
             out=x_last[:], in_=x_rows[LAST_ROWS[0] : LAST_ROWS[1], SHIFT : SHIFT + 2 * WINDOW, :]
         )
-        load_columns(0, ROUND_TILES - 1)
-        for r in range(1, ROUNDS):
-            load_columns(r * ROUND_TILES - 1, (r + 1) * ROUND_TILES - 1)
+        for j0, j1 in ((0, 2), (2, SHIFT), (SHIFT, 5), (5, WINDOW)):
+            load_columns(j0, j1)
         load_weights(0)
         load_weights(1)
         bias_bc = keep.tile([P, TENSORS * D], BF16)
@@ -137,22 +134,26 @@ def tile_successiveswintransfomerblock_pa_kernel(
         nc.vector.tensor_copy(out=gb_cols[:], in_=gb_bank[:, 0 : 2 * K_BLOCKS])
 
         sort_main = keep.tile([P, P], F32)
-        for b in range(IMAGES):
-            for window_row in range(GRID):
-                window = b * POSITIONS + window_row * GRID
-                for i0, r0, rows in cyclic_pieces(window_row * WINDOW - SHIFT, WINDOW, SIDE):
-                    row = b * SIDE + r0
-                    nc.vector.tensor_copy(
-                        out=sort_main[:, window * WINDOW + i0 : window * WINDOW + i0 + rows],
-                        in_=ident[:, EDGE_BASE + row : EDGE_BASE + row + rows],
-                    )
-                    if window + 2 < MAIN_WINDOWS:
-                        first = inner_partition(row)
-                        nc.vector.tensor_copy(
-                            out=sort_main[:, (window + 1) * WINDOW : (window + 3) * WINDOW]
-                            .rearrange("p (w i) -> p w i", w=2)[:, :, i0 : i0 + rows],
-                            in_=ident[:, first : first + 2 * rows].rearrange("p (i w) -> p w i", w=2),
-                        )
+        for row in range(0, IMAGES * SIDE, RUN):
+            image, r0 = divmod(row, SIDE)
+            window_row, i0 = divmod((r0 + SHIFT) % SIDE, WINDOW)
+            window = image * POSITIONS + window_row * GRID
+            columns = GRID if row < FULL_ROWS else 1
+            first = 4 * (row % FULL_ROWS)
+            lane = slice(0, GRID) if row < FULL_ROWS else slice(3, 4)
+            nc.vector.tensor_copy(
+                out=sort_main[:, window * WINDOW : (window + columns) * WINDOW]
+                .rearrange("p (w i) -> p w i", w=columns)[:, :, i0 : i0 + RUN],
+                in_=ident[:, first : first + 4 * RUN].rearrange("p (i c) -> p c i", c=4)[:, lane, :],
+            )
+            if row >= FULL_ROWS and window + 2 < MAIN_WINDOWS:
+                first = home(row, 1) - 3
+                nc.vector.tensor_copy(
+                    out=sort_main[:, (window + 1) * WINDOW : (window + 3) * WINDOW]
+                    .rearrange("p (w i) -> p w i", w=2)[:, :, i0 : i0 + RUN],
+                    in_=ident[:, first : first + 8 * RUN]
+                    .rearrange("p (i w c) -> p w i c", w=2, c=4)[:, :, :, 3],
+                )
         sort_last = keep.tile([P, P], F32)
         nc.vector.tensor_copy(
             out=sort_last[:].rearrange("p (i j w) -> p i j w", i=WINDOW, w=LAST_WINDOWS),

@@ -31,8 +31,7 @@ N_TILE = 512
 HALVES = D // N_TILE
 BANK_HEADS = N_TILE // HEAD_DIM
 TOKEN_TILES = IMAGES * SIDE * SIDE // P
-ROUND_TILES = 3
-ROUNDS = TOKEN_TILES // ROUND_TILES
+ROUND_TILES = (1, 4, 4)
 STATS_CHUNK = 512
 
 MAIN_WINDOWS = P // WINDOW
@@ -40,8 +39,6 @@ LAST_WINDOWS = IMAGES * POSITIONS - MAIN_WINDOWS
 LAST_ROWS = (SIDE + 2 * WINDOW - SHIFT, SIDE + 3 * WINDOW - SHIFT)
 FULL_ROWS = 32
 RUN = 4
-
-SCALAR_EVERY = 3
 
 FLOPS = 2 * IMAGES * SIDE * SIDE * D * TENSORS * D
 
@@ -63,9 +60,9 @@ def tile_successiveswintransfomerblock_pa_kernel(
 
     with ExitStack() as stack:
         keep = stack.enter_context(tc.tile_pool(name="keep", bufs=1))
-        small = stack.enter_context(tc.tile_pool(name="small", bufs=ROUNDS))
-        z_pool = stack.enter_context(tc.tile_pool(name="z_pool", bufs=2 * ROUND_TILES))
-        round_pool = stack.enter_context(tc.tile_pool(name="round_pool", bufs=2))
+        small = stack.enter_context(tc.tile_pool(name="small", bufs=3))
+        z_pool = stack.enter_context(tc.tile_pool(name="z_pool", bufs=6))
+        round_pool = stack.enter_context(tc.tile_pool(name="round_pool", bufs=3))
         w_pool = stack.enter_context(tc.tile_pool(name="w_pool", bufs=2 * PASSES))
         wg_pool = stack.enter_context(tc.tile_pool(name="wg_pool", bufs=4))
         stage_pool = stack.enter_context(tc.tile_pool(name="stage_pool", bufs=3))
@@ -99,40 +96,33 @@ def tile_successiveswintransfomerblock_pa_kernel(
         w_rows = Wqkv2.rearrange("(c t p) n -> c p t n", t=PACK, p=P)
         w_raw = {}
 
-        def load_weights(tensor):
+        def load_weights(first, count):
             for c in range(PASSES):
                 raw = w_pool.tile([P, PACK, D], BF16, name="w_raw")
-                nc.sync.dma_start(out=raw[:], in_=w_rows[c][:, :, tensor * D : (tensor + 1) * D])
-                w_raw[(tensor, c)] = raw
+                nc.sync.dma_start(out=raw[:], in_=w_rows[c][:, :, first * D : (first + count) * D])
+                for n in range(count):
+                    w_raw[(first + n, c)] = raw[:, :, n * D : (n + 1) * D]
 
+        bias_rows = keep.tile([P, TENSORS * D], BF16)
+        nc.vector.memset(bias_rows[:].bitcast(mybir.dt.int32), 0)
+        nc.gpsimd.dma_start(out=bias_rows[0:1, :], in_=bqkv2.rearrange("(o n) -> o n", o=1))
         gb_rows = keep.tile([P, P], BF16)
         nc.vector.memset(gb_rows[:], 0.0)
-        nc.scalar.dma_start(out=gb_rows[0:K_BLOCKS, :], in_=g3.rearrange("(r c) -> r c", c=P))
-        nc.scalar.dma_start(
+        nc.gpsimd.dma_start(out=gb_rows[0:K_BLOCKS, :], in_=g3.rearrange("(r c) -> r c", c=P))
+        nc.gpsimd.dma_start(
             out=gb_rows[K_BLOCKS : 2 * K_BLOCKS, :], in_=b3.rearrange("(r c) -> r c", c=P)
         )
 
-        nc.sync.dma_start(
-            out=x_last[:], in_=x_rows[LAST_ROWS[0] : LAST_ROWS[1], SHIFT : SHIFT + 2 * WINDOW, :]
-        )
-        for j0, j1 in ((0, 2), (2, SHIFT), (SHIFT, 5), (5, WINDOW)):
-            load_columns(j0, j1)
-        load_weights(0)
-        load_weights(1)
-        bias_bc = keep.tile([P, TENSORS * D], BF16)
-        nc.sync.dma_start(out=bias_bc[:], in_=bqkv2.partition_broadcast(P))
-        load_weights(2)
-        x_tiles = [x_last[:]] + [x_main[:, j, :] for j in range(WINDOW)]
+        columns_in_order = [4, 5, 6, 7, 0, 1, 2, 3]
+        def load_last():
+            nc.sync.dma_start(
+                out=x_last[:], in_=x_rows[LAST_ROWS[0] : LAST_ROWS[1], SHIFT : SHIFT + 2 * WINDOW, :]
+            )
+        x_tiles = [x_main[:, j, :] for j in columns_in_order] + [x_last[:]]
+        LAST = WINDOW
 
         ident = keep.tile([P, P], F32)
         make_identity(nc, ident[:])
-        gb_rows_f32 = keep.tile([P, P], F32)
-        nc.vector.tensor_copy(out=gb_rows_f32[:], in_=gb_rows[:])
-        gb_bank = psum.tile([P, N_TILE], F32, tag="flip")
-        nc.tensor.transpose(out=gb_bank[:, 0:P], in_=gb_rows_f32[:], identity=ident[:])
-        gb_cols = keep.tile([P, 2 * K_BLOCKS], F32)
-        nc.vector.tensor_copy(out=gb_cols[:], in_=gb_bank[:, 0 : 2 * K_BLOCKS])
-
         sort_main = keep.tile([P, P], F32)
         for row in range(0, IMAGES * SIDE, RUN):
             image, r0 = divmod(row, SIDE)
@@ -159,93 +149,157 @@ def tile_successiveswintransfomerblock_pa_kernel(
             out=sort_last[:].rearrange("p (i j w) -> p i j w", i=WINDOW, w=LAST_WINDOWS),
             in_=ident[:].rearrange("p (i w j) -> p i j w", i=WINDOW, w=LAST_WINDOWS),
         )
-        sorts = [sort_last] + [sort_main] * WINDOW
+        sorts = [sort_main] * WINDOW + [sort_last]
+        gb_cols = keep.tile([P, 2 * K_BLOCKS], F32)
+
+        def gain_and_bias():
+            gb_rows_f32 = keep.tile([P, P], F32)
+            nc.vector.tensor_copy(out=gb_rows_f32[:], in_=gb_rows[:])
+            gb_bank = psum.tile([P, N_TILE], F32, tag="flip")
+            nc.tensor.transpose(out=gb_bank[:, 0:P], in_=gb_rows_f32[:], identity=ident[:])
+            nc.vector.tensor_copy(out=gb_cols[:], in_=gb_bank[:, 0 : 2 * K_BLOCKS])
+
+        ones = keep.tile([P, P], BF16)
+        nc.vector.memset(ones[:], 1.0)
+        bias_bc = keep.tile([P, TENSORS * D], BF16)
+
+        def spread_bias(n):
+            cols = slice(n * N_TILE, (n + 1) * N_TILE)
+            bank = psum.tile([P, N_TILE], F32, name="acc", tag="acc")
+            nc.tensor.matmul(out=bank[:], lhsT=ones[:], rhs=bias_rows[:, cols], start=True, stop=True)
+            nc.scalar.copy(out=bias_bc[:, cols], in_=bank[:])
 
         mean_var = keep.tile([P, TOKEN_TILES, 2], F32)
         std = keep.tile([P, TOKEN_TILES], F32)
         rstd = keep.tile([P, TOKEN_TILES], F32)
         x_codes = keep.tile([P, PASSES, TOKEN_TILES * P], U32, align_bytes=64)
         x_scales = keep.tile([P, PASSES, TOKEN_TILES * P], U8, align_bytes=64)
-        width = ROUND_TILES * P
 
-        def statistics(r):
-            tiles = slice(r * ROUND_TILES, (r + 1) * ROUND_TILES)
-            stats = small.tile([P, ROUND_TILES, D // STATS_CHUNK, 6], F32, name="stats")
-            for a in range(ROUND_TILES):
-                for h in range(D // STATS_CHUNK):
-                    nc.vector.bn_stats(
-                        out=stats[:, a, h, :],
-                        in_=x_tiles[r * ROUND_TILES + a][:, h * STATS_CHUNK : (h + 1) * STATS_CHUNK],
-                    )
-                nc.vector.bn_aggr(
-                    out=mean_var[:, r * ROUND_TILES + a, :],
-                    in_=stats[:, a, :, :].rearrange("p h s -> p (h s)"),
-                )
-            nc.scalar.activation(
-                out=std[:, tiles], in_=mean_var[:, tiles, 1], func=ACT.Sqrt, bias=LN_EPS
+        stats_of = {}
+
+        def bh(a, h):
+            if h == 0:
+                stats_of[a] = small.tile([P, D // STATS_CHUNK, 6], F32, name="stats")
+            nc.vector.bn_stats(
+                out=stats_of[a][:, h, :], in_=x_tiles[a][:, h * STATS_CHUNK : (h + 1) * STATS_CHUNK]
             )
-            nc.vector.reciprocal(out=rstd[:, tiles], in_=std[:, tiles])
 
-        def normalise(r):
-            z_tiles = []
-            for a in range(r * ROUND_TILES, (r + 1) * ROUND_TILES):
-                z = z_pool.tile([P, D], F32, name="z")
-                nc.vector.tensor_scalar(
-                    out=z[:], in0=x_tiles[a],
-                    scalar1=mean_var[:, a, 0:1], scalar2=rstd[:, a : a + 1],
-                    op0=ALU.subtract, op1=ALU.mult,
-                )
-                z_tiles.append(z)
-            planes = round_pool.tile([P, K_BLOCKS, width], BF16, name="planes")
-            for j in range(K_BLOCKS):
+        def ag(a):
+            nc.vector.bn_aggr(
+                out=mean_var[:, a, :], in_=stats_of[a][:].rearrange("p h s -> p (h s)")
+            )
+
+        def vector_statistics(a):
+            bh(a, 0)
+            bh(a, 1)
+            ag(a)
+
+        minus_half = keep.tile([P, TOKEN_TILES], F32)
+        nc.gpsimd.memset(minus_half[:], -0.5)
+
+        def inverse_deviation(tiles):
+            part = slice(tiles[0], tiles[-1] + 1)
+            nc.gpsimd.tensor_scalar(
+                out=std[:, part], in0=mean_var[:, part, 1], scalar1=LN_EPS, scalar2=None, op0=ALU.add
+            )
+            nc.gpsimd.tensor_tensor(
+                out=rstd[:, part], in0=std[:, part], in1=minus_half[:, part], op=ALU.pow
+            )
+
+        z_tiles = {}
+
+        def centre(a):
+            z = z_pool.tile([P, D], F32, name="z")
+            nc.vector.tensor_scalar(
+                out=z[:], in0=x_tiles[a],
+                scalar1=mean_var[:, a, 0:1], scalar2=rstd[:, a : a + 1],
+                op0=ALU.subtract, op1=ALU.mult,
+            )
+            z_tiles[a] = z
+
+        shift = keep.tile([P, TOKEN_TILES], F32)
+
+        def centre_by_scalar(a):
+            z = z_pool.tile([P, D], F32, name="z")
+            nc.gpsimd.tensor_tensor(
+                out=shift[:, a : a + 1], in0=mean_var[:, a, 0:1], in1=rstd[:, a : a + 1], op=ALU.mult
+            )
+            nc.gpsimd.tensor_scalar(
+                out=shift[:, a : a + 1], in0=shift[:, a : a + 1], scalar1=-1.0, scalar2=None, op0=ALU.mult
+            )
+            nc.scalar.activation(
+                out=z[:], in_=x_tiles[a], func=ACT.Identity,
+                scale=rstd[:, a : a + 1], bias=shift[:, a : a + 1],
+            )
+            z_tiles[a] = z
+
+        planes = {}
+
+        def flip(tiles, c):
+            width = len(tiles) * P
+            plane = round_pool.tile([P, PACK, width], BF16, name="plane")
+            for t in range(PACK):
+                j = c * PACK + t
                 bank = psum.tile([P, N_TILE], F32, name="flipped", tag="flip")
-                for a in range(ROUND_TILES):
+                for n, a in enumerate(tiles):
                     nc.tensor.transpose(
-                        out=bank[:, a * P : (a + 1) * P],
+                        out=bank[:, n * P : (n + 1) * P],
                         in_=z_tiles[a][:, j * P : (j + 1) * P],
-                        identity=sorts[r * ROUND_TILES + a][:],
+                        identity=sorts[a][:],
                     )
                 nc.scalar.activation(
-                    out=planes[:, j, :], in_=bank[:, 0:width],
+                    out=plane[:, t, :], in_=bank[:, 0:width],
                     func=ACT.Identity, scale=gb_cols[:, j : j + 1],
                     bias=gb_cols[:, K_BLOCKS + j : K_BLOCKS + j + 1],
                 )
-            grouped = round_pool.tile([P, PASSES, width, PACK], BF16, name="x_grouped", align_bytes=64)
-            for c in range(PASSES):
-                nc.vector.tensor_copy(
-                    out=grouped[:, c, :, :].rearrange("p (n i) t -> p n t i", i=4),
-                    in_=planes[:, c * PACK : (c + 1) * PACK, :].rearrange("p t (n i) -> p n t i", i=4),
-                )
-            for c in range(PASSES):
-                for a in range(ROUND_TILES):
-                    cols = slice((r * ROUND_TILES + a) * P, (r * ROUND_TILES + a + 1) * P)
-                    nc.vector.quantize_mx(
-                        out=x_codes[:, c, cols].bitcast(FP8X4),
-                        scales=x_scales[:, c, cols],
-                        in_=grouped[:, c, a * P : (a + 1) * P, :].rearrange("p m t -> p (m t)"),
-                    )
+            planes[(tiles[0], c)] = plane
+
+        x_grouped = {}
+
+        def group(tiles, c):
+            grouped = round_pool.tile([P, len(tiles) * P, PACK], BF16, name="grouped", align_bytes=64)
+            nc.vector.tensor_copy(
+                out=grouped[:].rearrange("p (n i) t -> p n t i", i=4),
+                in_=planes[(tiles[0], c)][:].rearrange("p t (n i) -> p n t i", i=4),
+            )
+            x_grouped[(tiles[0], c)] = grouped
+
+        def quantise(tiles, c):
+            cols = slice(tiles[0] * P, (tiles[-1] + 1) * P)
+            nc.vector.quantize_mx(
+                out=x_codes[:, c, cols].bitcast(FP8X4),
+                scales=x_scales[:, c, cols],
+                in_=x_grouped[(tiles[0], c)][:].rearrange("p m t -> p (m t)"),
+            )
 
         w_codes = keep.tile([P, PASSES, TENSORS * D], U32, align_bytes=64)
         w_scales = keep.tile([P, PASSES, TENSORS * D], U8, align_bytes=64)
+        w_grouped = {}
 
-        def quantise_weights(tensor):
-            for half in range(HALVES):
-                for c in range(PASSES):
-                    rows = w_raw[(tensor, c)][:, :, half * N_TILE : (half + 1) * N_TILE]
-                    grouped = wg_pool.tile([P, N_TILE, PACK], BF16, name="w_grouped", align_bytes=64)
-                    copy = nc.vector.tensor_copy if tensor == 0 and c == 0 else nc.scalar.copy
-                    copy(
-                        out=grouped[:].rearrange("p (n i) t -> p n t i", i=4),
-                        in_=rows.rearrange("p t (n i) -> p n t i", i=4),
-                    )
-                    cols = slice(tensor * D + half * N_TILE, tensor * D + (half + 1) * N_TILE)
-                    nc.vector.quantize_mx(
-                        out=w_codes[:, c, cols].bitcast(FP8X4),
-                        scales=w_scales[:, c, cols],
-                        in_=grouped[:].rearrange("p n t -> p (n t)"),
-                    )
+        def group_weights(tensor, half, c, engine):
+            rows = w_raw[(tensor, c)][:, :, half * N_TILE : (half + 1) * N_TILE]
+            grouped = wg_pool.tile([P, N_TILE, PACK], BF16, name="w_group", align_bytes=64)
+            side_by_side = grouped[:].rearrange("p (n i) t -> p n t i", i=4)
+            rows = rows.rearrange("p t (n i) -> p n t i", i=4)
+            if engine == "V":
+                nc.vector.tensor_copy(out=side_by_side, in_=rows)
+            elif engine == "G":
+                nc.gpsimd.tensor_scalar(
+                    out=side_by_side, in0=rows, scalar1=1.0, scalar2=0.0, op0=ALU.mult, op1=ALU.add
+                )
+            else:
+                nc.scalar.copy(out=side_by_side, in_=rows)
+            w_grouped[(tensor, half, c)] = grouped
 
-        def project(a, tensor, half, target, by_scalar):
+        def quantise_weights(tensor, half, c):
+            cols = slice(tensor * D + half * N_TILE, tensor * D + (half + 1) * N_TILE)
+            nc.vector.quantize_mx(
+                out=w_codes[:, c, cols].bitcast(FP8X4),
+                scales=w_scales[:, c, cols],
+                in_=w_grouped[(tensor, half, c)][:].rearrange("p n t -> p (n t)"),
+            )
+
+        def project(a, tensor, half):
             tokens = slice(a * P, (a + 1) * P)
             cols = slice(tensor * D + half * N_TILE, tensor * D + (half + 1) * N_TILE)
             acc = psum.tile([P, N_TILE], F32, name="acc", tag="acc")
@@ -259,6 +313,10 @@ def tile_successiveswintransfomerblock_pa_kernel(
                     start=(c == 0),
                     stop=(c == PASSES - 1),
                 )
+            return acc
+
+        def empty(acc, tensor, half, target, by_scalar):
+            cols = slice(tensor * D + half * N_TILE, tensor * D + (half + 1) * N_TILE)
             product = acc[:].rearrange("p (h d) -> p h d", d=HEAD_DIM)
             bias = bias_bc[:, cols].rearrange("p (h d) -> p h d", d=HEAD_DIM)
             if by_scalar:
@@ -267,39 +325,85 @@ def tile_successiveswintransfomerblock_pa_kernel(
             else:
                 nc.vector.tensor_tensor(out=target, in0=product, in1=bias, op=ALU.add)
 
-        def project_last(tensor):
-            stage = last_pool.tile([P, HEADS, HEAD_DIM], F32, name="stage_last")
-            for half in range(HALVES):
-                heads = slice(half * BANK_HEADS, (half + 1) * BANK_HEADS)
-                project(0, tensor, half, stage[:, heads, :], False)
+        def store_last(tensor, stage):
             for w in range(LAST_WINDOWS):
                 nc.sync.dma_start(
                     out=outs[tensor][MAIN_WINDOWS + w].rearrange("h n d -> n h d"),
                     in_=stage[w:P:LAST_WINDOWS],
                 )
 
-        def project_main(tensor, half):
-            stage = stage_pool.tile([P, BANK_HEADS, WINDOW, HEAD_DIM], F32, name="stage")
-            for j in range(WINDOW):
-                project(
-                    1 + j, tensor, half, stage[:, :, j, :], j % SCALAR_EVERY == SCALAR_EVERY - 1
-                )
+        def store_main(tensor, half, j0=0, j1=WINDOW):
+            part = False
+            stage = stages[(tensor, half, 0 if j0 else 1)] if part else stages[(tensor, half)]
             for h in range(BANK_HEADS):
+                head = outs[tensor][0:MAIN_WINDOWS, half * BANK_HEADS + h, :, :].rearrange(
+                    "w (i j) d -> w i j d", j=WINDOW
+                )
                 nc.sync.dma_start(
-                    out=outs[tensor][0:MAIN_WINDOWS, half * BANK_HEADS + h, :, :].rearrange(
-                        "w (i j) d -> w i (j d)", j=WINDOW
-                    ),
-                    in_=stage[:, h, :, :].rearrange("p j d -> p (j d)"),
+                    out=head[:, :, j0:j1, :].rearrange("w i j d -> w i (j d)"),
+                    in_=(stage[:, h, :, :] if part else stage[:, h, j0:j1, :]).rearrange("p j d -> p (j d)"),
                 )
 
-        for r in range(ROUNDS):
-            statistics(r)
-        for r in range(ROUNDS):
-            normalise(r)
-        quantise_weights(0)
-        for tensor in range(TENSORS):
-            project_last(tensor)
-            for half in range(HALVES):
-                project_main(tensor, half)
-            if tensor + 1 < TENSORS:
-                quantise_weights(tensor + 1)
+        stages = {}
+
+        PARTS = [0]
+        SB = 4
+        A, B, C, E, L = [0, 1], [2, 3], [4, 5], [6, 7], [8]
+        bn, rs, ce, fl, gr, qu = vector_statistics, inverse_deviation, centre, flip, group, quantise
+        gw, qw, sb = group_weights, quantise_weights, spread_bias
+        stack.enter_context(tc.manual_schedule())
+        load_columns(4, 6)
+        load_columns(6, 8)
+        load_columns(0, 2)
+        load_weights(0, 1)
+        load_columns(2, 4)
+        load_last()
+        load_weights(1, 1)
+        load_weights(2, 1)
+        for n in range(6): sb(n)
+        cs = centre_by_scalar
+        bh(0, 0); bh(0, 1); bh(1, 0); ag(0); bh(1, 1); bh(2, 0); ag(1); rs(A); gain_and_bias(); bh(2, 1)
+        ce(0); cs(1); fl(A, 0); fl(A, 1)
+        bh(3, 0); ag(2); bh(3, 1)
+        bh(4, 0); ag(3); rs(B); bh(4, 1)
+        gr(A, 0); ag(4); ce(2); cs(3); qu(A, 0); gr(A, 1); fl(B, 0); fl(B, 1)
+        bh(5, 0); qu(A, 1); bh(5, 1)
+        gw(0, 0, 0, "V"); ag(5); rs(C)
+        bh(6, 0)
+        gr(B, 0); ce(4); cs(5); gr(B, 1); qu(B, 0); fl(C, 0); fl(C, 1)
+        bh(6, 1); qu(B, 1); qw(0, 0, 0)
+        bh(7, 0); ag(6); bh(7, 1)
+        gw(0, 0, 1, "V"); ag(7); rs(E)
+        gr(C, 0); bh(8, 0); ce(6); cs(7); gr(C, 1); qu(C, 0); fl(E, 0); fl(E, 1)
+        qw(0, 0, 1); qu(C, 1)
+        bh(8, 1)
+        gw(0, 1, 0, "S")
+        ag(8); rs(L)
+        gw(0, 1, 1, "V")
+        gr(E, 0); ce(8); fl(L, 0); fl(L, 1); gr(E, 1); qu(E, 0)
+
+        todo = [(n, 0, h) for h in range(2) for n in range(8)] + [(8, 0, 0), (8, 0, 1)] + [(n, t, h) for t in range(1, 3) for h in range(2) for n in range(9)]
+        background = {0: [(qu, E, 1)], 1: [(qw, 0, 1, 1), (gr, L, 0)], 2: [(gr, L, 1), (gw, 1, 0, 0, "S")], 3: [(qw, 0, 1, 0)], 4: [(qu, L, 0), (qu, L, 1), (gw, 1, 0, 1, "S")], 8: [(qw, 1, 0, 0)], 10: [(gw, 1, 1, 0, "S")], 13: [(qw, 1, 0, 1), (gw, 1, 1, 1, "S")], 16: [(qw, 1, 1, 0)], 19: [(qw, 1, 1, 1), (gw, 2, 0, 0, "S")], 23: [(gw, 2, 0, 1, "S"), (qw, 2, 0, 0)], 27: [(gw, 2, 1, 0, "S"), (qw, 2, 0, 1)], 31: [(gw, 2, 1, 1, "S"), (qw, 2, 1, 0)], 35: [(qw, 2, 1, 1)]}
+        def target_of(n, t, h):
+            if n == LAST:
+                if (t, "last") not in stages:
+                    stages[(t, "last")] = last_pool.tile([P, HEADS, HEAD_DIM], F32, name="stage_last")
+                return stages[(t, "last")][:, h * BANK_HEADS : (h + 1) * BANK_HEADS, :]
+            if (t, h) not in stages:
+                stages[(t, h)] = stage_pool.tile([P, BANK_HEADS, WINDOW, HEAD_DIM], F32, name="stage", bufs=SB)
+            return stages[(t, h)][:, :, columns_in_order[n], :]
+        open_banks = []
+        def finish():
+            i, n, t, h, acc = open_banks.pop(0)
+            empty(acc, t, h, target_of(n, t, h), (lambda i: i >= 36 and i % 2 == 1)(i))
+            if n == 3 and t in PARTS: store_main(t, h, 4, 8)
+            if n == 7:
+                if t in PARTS: store_main(t, h, 0, 4)
+                else: store_main(t, h)
+            if n == 8 and h == 1: store_last(t, stages[(t, "last")])
+        for i, (n, t, h) in enumerate(todo):
+            open_banks.append((i, n, t, h, project(n, t, h)))
+            for step in background.get(i, []):
+                step[0](*step[1:])
+            if len(open_banks) > 2: finish()
+        while open_banks: finish()

@@ -105,15 +105,17 @@ def tile_successiveswintransfomerblock_pa_kernel(
 
         bias_rows = keep.tile([P, TENSORS * D], BF16)
         nc.vector.memset(bias_rows[:].bitcast(mybir.dt.int32), 0)
-        nc.gpsimd.dma_start(out=bias_rows[0:1, :], in_=bqkv2.rearrange("(o n) -> o n", o=1))
         gb_rows = keep.tile([P, P], BF16)
         nc.vector.memset(gb_rows[:], 0.0)
-        nc.gpsimd.dma_start(out=gb_rows[0:K_BLOCKS, :], in_=g3.rearrange("(r c) -> r c", c=P))
-        nc.gpsimd.dma_start(
-            out=gb_rows[K_BLOCKS : 2 * K_BLOCKS, :], in_=b3.rearrange("(r c) -> r c", c=P)
-        )
 
         columns_in_order = [4, 5, 6, 7, 0, 1, 2, 3]
+        def load_vectors():
+            nc.sync.dma_start(out=bias_rows[0:1, :], in_=bqkv2.rearrange("(o n) -> o n", o=1))
+            nc.sync.dma_start(out=gb_rows[0:K_BLOCKS, :], in_=g3.rearrange("(r c) -> r c", c=P))
+            nc.sync.dma_start(
+                out=gb_rows[K_BLOCKS : 2 * K_BLOCKS, :], in_=b3.rearrange("(r c) -> r c", c=P)
+            )
+
         def load_last():
             nc.sync.dma_start(
                 out=x_last[:], in_=x_rows[LAST_ROWS[0] : LAST_ROWS[1], SHIFT : SHIFT + 2 * WINDOW, :]
@@ -353,6 +355,7 @@ def tile_successiveswintransfomerblock_pa_kernel(
         gw, qw, sb = group_weights, quantise_weights, spread_bias
         stack.enter_context(tc.manual_schedule())
         load_columns(4, 6)
+        load_vectors()
         load_columns(6, 8)
         load_columns(0, 2)
         load_weights(0, 1)

@@ -334,75 +334,62 @@ def tile_successiveswintransfomerblock_pa_kernel(
                     in_=stage[w:P:LAST_WINDOWS],
                 )
 
-        def store_main(tensor, half, j0=0, j1=WINDOW):
-            part = False
-            stage = stages[(tensor, half, 0 if j0 else 1)] if part else stages[(tensor, half)]
+        def store_part(tensor, half, part):
+            j0 = columns_in_order[4 * part]
+            stage = stages[(tensor, half, part)]
             for h in range(BANK_HEADS):
                 head = outs[tensor][0:MAIN_WINDOWS, half * BANK_HEADS + h, :, :].rearrange(
                     "w (i j) d -> w i j d", j=WINDOW
                 )
                 nc.sync.dma_start(
-                    out=head[:, :, j0:j1, :].rearrange("w i j d -> w i (j d)"),
-                    in_=(stage[:, h, :, :] if part else stage[:, h, j0:j1, :]).rearrange("p j d -> p (j d)"),
+                    out=head[:, :, j0 : j0 + 4, :].rearrange("w i j d -> w i (j d)"),
+                    in_=stage[:, h, :, :].rearrange("p j d -> p (j d)"),
                 )
 
         stages = {}
 
-        PARTS = [0]
-        SB = 4
+        SB = 7
         A, B, C, E, L = [0, 1], [2, 3], [4, 5], [6, 7], [8]
-        bn, rs, ce, fl, gr, qu = vector_statistics, inverse_deviation, centre, flip, group, quantise
+        rs, ce, cs, fl, gr, qu = inverse_deviation, centre, centre_by_scalar, flip, group, quantise
         gw, qw, sb = group_weights, quantise_weights, spread_bias
         stack.enter_context(tc.manual_schedule())
         load_columns(4, 6)
         load_vectors()
         load_columns(6, 8)
-        load_columns(0, 2)
         load_weights(0, 1)
+        load_weights(1, 1)
+        load_columns(0, 2)
         load_columns(2, 4)
         load_last()
-        load_weights(1, 1)
         load_weights(2, 1)
         for n in range(6): sb(n)
-        cs = centre_by_scalar
         bh(0, 0); bh(0, 1); bh(1, 0); ag(0); bh(1, 1); bh(2, 0); ag(1); rs(A); gain_and_bias(); bh(2, 1)
         ce(0); cs(1); fl(A, 0); fl(A, 1)
-        bh(3, 0); ag(2); bh(3, 1)
-        bh(4, 0); ag(3); rs(B); bh(4, 1)
-        gr(A, 0); ag(4); ce(2); cs(3); qu(A, 0); gr(A, 1); fl(B, 0); fl(B, 1)
-        bh(5, 0); qu(A, 1); bh(5, 1)
-        gw(0, 0, 0, "V"); ag(5); rs(C)
-        bh(6, 0)
-        gr(B, 0); ce(4); cs(5); gr(B, 1); qu(B, 0); fl(C, 0); fl(C, 1)
-        bh(6, 1); qu(B, 1); qw(0, 0, 0)
-        bh(7, 0); ag(6); bh(7, 1)
-        gw(0, 0, 1, "V"); ag(7); rs(E)
-        gr(C, 0); bh(8, 0); ce(6); cs(7); gr(C, 1); qu(C, 0); fl(E, 0); fl(E, 1)
-        qw(0, 0, 1); qu(C, 1)
-        bh(8, 1)
+        bh(3, 0); ag(2); bh(3, 1); ag(3); rs(B)
+        gw(0, 0, 0, "V")
+        gr(A, 0); ce(2); cs(3); fl(B, 0); fl(B, 1)
+        gr(A, 1); qu(A, 0); gw(0, 0, 1, "V"); qu(A, 1)
+        qw(0, 0, 0); qw(0, 0, 1)
+        gr(B, 0); gr(B, 1); qu(B, 0); qu(B, 1)
         gw(0, 1, 0, "S")
-        ag(8); rs(L)
-        gw(0, 1, 1, "V")
-        gr(E, 0); ce(8); fl(L, 0); fl(L, 1); gr(E, 1); qu(E, 0)
 
-        todo = [(n, 0, h) for h in range(2) for n in range(8)] + [(8, 0, 0), (8, 0, 1)] + [(n, t, h) for t in range(1, 3) for h in range(2) for n in range(9)]
-        background = {0: [(qu, E, 1)], 1: [(qw, 0, 1, 1), (gr, L, 0)], 2: [(gr, L, 1), (gw, 1, 0, 0, "S")], 3: [(qw, 0, 1, 0)], 4: [(qu, L, 0), (qu, L, 1), (gw, 1, 0, 1, "S")], 8: [(qw, 1, 0, 0)], 10: [(gw, 1, 1, 0, "S")], 13: [(qw, 1, 0, 1), (gw, 1, 1, 1, "S")], 16: [(qw, 1, 1, 0)], 19: [(qw, 1, 1, 1), (gw, 2, 0, 0, "S")], 23: [(gw, 2, 0, 1, "S"), (qw, 2, 0, 0)], 27: [(gw, 2, 1, 0, "S"), (qw, 2, 0, 1)], 31: [(gw, 2, 1, 1, "S"), (qw, 2, 1, 0)], 35: [(qw, 2, 1, 1)]}
+        todo = [(n, t, h) for t in range(3) for h in range(2) for n in range(4)] + [(n, 0, h) for h in range(2) for n in range(4, 8)] + [(8, 0, 0), (8, 0, 1)] + [(n, 1, h) for h in range(2) for n in range(4, 8)] + [(8, 1, 0), (8, 1, 1)] + [(n, 2, 0) for n in range(4, 8)] + [(8, 2, 0), (8, 2, 1)] + [(n, 2, 1) for n in range(4, 8)]
+        background = {1: [(gw, 0, 1, 1, "V"), (gw, 1, 0, 0, "S")], 2: [(qw, 0, 1, 0)], 3: [(qw, 0, 1, 1), (gw, 1, 0, 1, "S")], 4: [(bh, 4, 0), (gw, 1, 1, 0, "S")], 5: [(bh, 4, 1)], 6: [(ag, 4), (qw, 1, 0, 0), (gw, 1, 1, 1, "S")], 7: [(qw, 1, 0, 1)], 8: [(bh, 5, 0)], 9: [(bh, 5, 1), (gw, 2, 0, 0, "S")], 10: [(ag, 5), (rs, C), (qw, 1, 1, 0), (gw, 2, 0, 1, "S")], 11: [(qw, 1, 1, 1)],
+ 12: [(ce, 4), (cs, 5), (fl, C, 0), (fl, C, 1)], 13: [(bh, 6, 0)], 14: [(bh, 6, 1), (qw, 2, 0, 0), (gw, 2, 1, 0, "S")], 15: [(ag, 6), (qw, 2, 0, 1), (gw, 2, 1, 1, "S")], 16: [(gr, C, 0), (bh, 7, 0)], 17: [(gr, C, 1), (qu, C, 0)], 18: [(bh, 7, 1), (qw, 2, 1, 0)], 19: [(ag, 7), (rs, E), (qw, 2, 1, 1), (qu, C, 1)], 20: [(ce, 6), (cs, 7), (fl, E, 0), (fl, E, 1)], 21: [(bh, 8, 0), (bh, 8, 1)], 22: [(ag, 8), (rs, L)], 23: [(gr, E, 0), (gr, E, 1)], 24: [(qu, E, 0), (ce, 8), (fl, L, 0), (fl, L, 1)], 25: [(qu, E, 1)], 27: [(gr, L, 0)], 28: [(gr, L, 1), (qu, L, 0)], 29: [(qu, L, 1)]}
         def target_of(n, t, h):
             if n == LAST:
                 if (t, "last") not in stages:
                     stages[(t, "last")] = last_pool.tile([P, HEADS, HEAD_DIM], F32, name="stage_last")
                 return stages[(t, "last")][:, h * BANK_HEADS : (h + 1) * BANK_HEADS, :]
-            if (t, h) not in stages:
-                stages[(t, h)] = stage_pool.tile([P, BANK_HEADS, WINDOW, HEAD_DIM], F32, name="stage", bufs=SB)
-            return stages[(t, h)][:, :, columns_in_order[n], :]
+            key = (t, h, n // 4)
+            if key not in stages:
+                stages[key] = stage_pool.tile([P, BANK_HEADS, WINDOW // 2, HEAD_DIM], F32, name="part", bufs=SB)
+            return stages[key][:, :, n % 4, :]
         open_banks = []
         def finish():
             i, n, t, h, acc = open_banks.pop(0)
-            empty(acc, t, h, target_of(n, t, h), (lambda i: i >= 36 and i % 2 == 1)(i))
-            if n == 3 and t in PARTS: store_main(t, h, 4, 8)
-            if n == 7:
-                if t in PARTS: store_main(t, h, 0, 4)
-                else: store_main(t, h)
+            empty(acc, t, h, target_of(n, t, h), (lambda i: i >= 24 and i % 2 == 1)(i))
+            if n % 4 == 3 and n < 8: store_part(t, h, n // 4)
             if n == 8 and h == 1: store_last(t, stages[(t, "last")])
         for i, (n, t, h) in enumerate(todo):
             open_banks.append((i, n, t, h, project(n, t, h)))

@@ -388,7 +388,7 @@ def tile_successiveswintransfomerblock_pa_kernel(
         open_banks = []
         def finish():
             i, n, t, h, acc = open_banks.pop(0)
-            empty(acc, t, h, target_of(n, t, h), (lambda i: i >= 24 and i % 2 == 1)(i))
+            empty(acc, t, h, target_of(n, t, h), (lambda i: False)(i))
             if n % 4 == 3 and n < 8: store_part(t, h, n // 4)
             if n == 8 and h == 1: store_last(t, stages[(t, "last")])
         for i, (n, t, h) in enumerate(todo):

@@ -334,21 +334,19 @@ def tile_successiveswintransfomerblock_pa_kernel(
                     in_=stage[w:P:LAST_WINDOWS],
                 )
 
-        def store_part(tensor, half, part):
-            j0 = columns_in_order[4 * part]
-            stage = stages[(tensor, half, part)]
+        def store_main(tensor, half, key, j0, j1):
+            stage = stages[key]
             for h in range(BANK_HEADS):
                 head = outs[tensor][0:MAIN_WINDOWS, half * BANK_HEADS + h, :, :].rearrange(
                     "w (i j) d -> w i j d", j=WINDOW
                 )
                 nc.sync.dma_start(
-                    out=head[:, :, j0 : j0 + 4, :].rearrange("w i j d -> w i (j d)"),
+                    out=head[:, :, j0:j1, :].rearrange("w i j d -> w i (j d)"),
                     in_=stage[:, h, :, :].rearrange("p j d -> p (j d)"),
                 )
 
         stages = {}
 
-        SB = 7
         A, B, C, E, L = [0, 1], [2, 3], [4, 5], [6, 7], [8]
         rs, ce, cs, fl, gr, qu = inverse_deviation, centre, centre_by_scalar, flip, group, quantise
         gw, qw, sb = group_weights, quantise_weights, spread_bias
@@ -373,26 +371,42 @@ def tile_successiveswintransfomerblock_pa_kernel(
         gr(B, 0); gr(B, 1); qu(B, 0); qu(B, 1)
         gw(0, 1, 0, "S")
 
-        todo = [(n, t, h) for t in range(3) for h in range(2) for n in range(4)] + [(n, 0, h) for h in range(2) for n in range(4, 8)] + [(8, 0, 0), (8, 0, 1)] + [(n, 1, h) for h in range(2) for n in range(4, 8)] + [(8, 1, 0), (8, 1, 1)] + [(n, 2, 0) for n in range(4, 8)] + [(8, 2, 0), (8, 2, 1)] + [(n, 2, 1) for n in range(4, 8)]
-        background = {1: [(gw, 0, 1, 1, "V"), (gw, 1, 0, 0, "S")], 2: [(qw, 0, 1, 0)], 3: [(qw, 0, 1, 1), (gw, 1, 0, 1, "S")], 4: [(bh, 4, 0), (gw, 1, 1, 0, "S")], 5: [(bh, 4, 1)], 6: [(ag, 4), (qw, 1, 0, 0), (gw, 1, 1, 1, "S")], 7: [(qw, 1, 0, 1)], 8: [(bh, 5, 0)], 9: [(bh, 5, 1), (gw, 2, 0, 0, "S")], 10: [(ag, 5), (rs, C), (qw, 1, 1, 0), (gw, 2, 0, 1, "S")], 11: [(qw, 1, 1, 1)],
- 12: [(ce, 4), (cs, 5), (fl, C, 0), (fl, C, 1)], 13: [(bh, 6, 0)], 14: [(bh, 6, 1), (qw, 2, 0, 0), (gw, 2, 1, 0, "S")], 15: [(ag, 6), (qw, 2, 0, 1), (gw, 2, 1, 1, "S")], 16: [(gr, C, 0), (bh, 7, 0)], 17: [(gr, C, 1), (qu, C, 0)], 18: [(bh, 7, 1), (qw, 2, 1, 0)], 19: [(ag, 7), (rs, E), (qw, 2, 1, 1), (qu, C, 1)], 20: [(ce, 6), (cs, 7), (fl, E, 0), (fl, E, 1)], 21: [(bh, 8, 0), (bh, 8, 1)], 22: [(ag, 8), (rs, L)], 23: [(gr, E, 0), (gr, E, 1)], 24: [(qu, E, 0), (ce, 8), (fl, L, 0), (fl, L, 1)], 25: [(qu, E, 1)], 27: [(gr, L, 0)], 28: [(gr, L, 1), (qu, L, 0)], 29: [(qu, L, 1)]}
+        todo = [(n, t, h) for t in range(2) for h in range(2) for n in range(4)] + [(n, t, h) for t in range(2) for pair in ((4, 5), (6, 7)) for h in range(2) for n in pair] + [(8, t, h) for t in range(2) for h in range(2)] + [(n, 2, 0) for n in range(8)] + [(8, 2, 0), (8, 2, 1)] + [(n, 2, 1) for n in range(8)]
+        background = {1: [(gw, 0, 1, 1, "V"), (gw, 1, 0, 0, "S")], 2: [(qw, 0, 1, 0)], 3: [(qw, 0, 1, 1), (gw, 1, 0, 1, "S")], 4: [(bh, 4, 0), (gw, 1, 1, 0, "S")], 5: [(bh, 4, 1)], 6: [(ag, 4), (qw, 1, 0, 0), (gw, 1, 1, 1, "S")], 7: [(qw, 1, 0, 1)], 8: [(bh, 5, 0)], 9: [(bh, 5, 1)], 10: [(ag, 5), (rs, C), (qw, 1, 1, 0)], 11: [(qw, 1, 1, 1), (bh, 6, 0)], 12: [(ce, 4), (cs, 5), (fl, C, 0), (fl, C, 1), (bh, 6, 1)], 13: [(bh, 7, 0), (ag, 6), (bh, 7, 1)], 14: [(ag, 7), (rs, E)], 15: [(gr, C, 0), (ce, 6), (cs, 7), (fl, E, 0), (fl, E, 1), (gr, C, 1), (qu, C, 0), (qu, C, 1)],
+ 18: [(gr, E, 0), (bh, 8, 0), (gr, E, 1), (qu, E, 0)], 19: [(qu, E, 1), (gw, 2, 0, 0, "S")], 21: [(bh, 8, 1), (gw, 2, 0, 1, "S")], 22: [(ag, 8), (rs, L)], 23: [(gw, 2, 1, 0, "S")], 24: [(ce, 8)], 25: [(gw, 2, 1, 1, "S"), (fl, L, 0), (fl, L, 1)], 26: [(qw, 2, 0, 0)], 28: [(qw, 2, 0, 1)], 29: [(gr, L, 0)], 30: [(gr, L, 1), (qu, L, 0)], 31: [(qu, L, 1)], 33: [(qw, 2, 1, 0)], 35: [(qw, 2, 1, 1)]}
         def target_of(n, t, h):
             if n == LAST:
                 if (t, "last") not in stages:
                     stages[(t, "last")] = last_pool.tile([P, HEADS, HEAD_DIM], F32, name="stage_last")
                 return stages[(t, "last")][:, h * BANK_HEADS : (h + 1) * BANK_HEADS, :]
-            key = (t, h, n // 4)
-            if key not in stages:
-                stages[key] = stage_pool.tile([P, BANK_HEADS, WINDOW // 2, HEAD_DIM], F32, name="part", bufs=SB)
-            return stages[key][:, :, n % 4, :]
+            if t < 2:
+                key = (t, h, n // 4)
+                if key not in stages:
+                    stages[key] = stage_pool.tile([P, BANK_HEADS, WINDOW // 2, HEAD_DIM], F32, name="part", bufs=4)
+                return stages[key][:, :, n % 4, :]
+            if (t, h) not in stages:
+                stages[(t, h)] = stage_pool.tile([P, BANK_HEADS, WINDOW, HEAD_DIM], F32, name="stage", bufs=2)
+            return stages[(t, h)][:, :, columns_in_order[n], :]
         open_banks = []
+        left = {}
+        for n, t, h in todo:
+            key = (t, "last") if n == LAST else (t, h, n // 4) if t < 2 else (t, h)
+            left[key] = left.get(key, 0) + 1
         def finish():
-            i, n, t, h, acc = open_banks.pop(0)
-            empty(acc, t, h, target_of(n, t, h), (lambda i: False)(i))
-            if n % 4 == 3 and n < 8: store_part(t, h, n // 4)
-            if n == 8 and h == 1: store_last(t, stages[(t, "last")])
+            n, t, h, acc = open_banks.pop(0)
+            empty(acc, t, h, target_of(n, t, h), False)
+            key = (t, "last") if n == LAST else (t, h, n // 4) if t < 2 else (t, h)
+            left[key] -= 1
+            if left[key] == 0:
+                if n == LAST:
+                    store_last(t, stages[key])
+                elif t < 2:
+                    j0 = columns_in_order[n // 4 * 4]
+                    store_main(t, h, key, j0, j0 + 4)
+                else:
+                    store_main(t, h, key, 0, WINDOW)
         for i, (n, t, h) in enumerate(todo):
-            open_banks.append((i, n, t, h, project(n, t, h)))
+            open_banks.append((n, t, h, project(n, t, h)))
             for step in background.get(i, []):
                 step[0](*step[1:])
             if len(open_banks) > 2: finish()

from contextlib import ExitStack

import concourse.mybir as mybir
from concourse.masks import make_identity

FP8X4 = mybir.dt.float8_e4m3fn_x4
BF16 = mybir.dt.bfloat16
F32 = mybir.dt.float32
U32 = mybir.dt.uint32
U8 = mybir.dt.uint8
ACT = mybir.ActivationFunctionType
ALU = mybir.AluOpType

P = 128
IMAGES = 2
SIDE = 24
WINDOW = 8
SHIFT = 4
GRID = SIDE // WINDOW
POSITIONS = GRID * GRID
D = 1024
HEADS = 16
HEAD_DIM = 64
TENSORS = 3
LN_EPS = 1e-5

PACK = 4
PASSES = D // (P * PACK)
K_BLOCKS = D // P
N_TILE = 512
HALVES = D // N_TILE
BANK_HEADS = N_TILE // HEAD_DIM
TOKEN_TILES = IMAGES * SIDE * SIDE // P
ROUND_TILES = (1, 4, 4)
STATS_CHUNK = 512

MAIN_WINDOWS = P // WINDOW
LAST_WINDOWS = IMAGES * POSITIONS - MAIN_WINDOWS
LAST_ROWS = (SIDE + 2 * WINDOW - SHIFT, SIDE + 3 * WINDOW - SHIFT)
FULL_ROWS = 32
RUN = 4

FLOPS = 2 * IMAGES * SIDE * SIDE * D * TENSORS * D


def home(row, column):
    if row < FULL_ROWS:
        return 4 * row + column
    if column == 0:
        return 4 * (row - FULL_ROWS) + 3
    run_start = 16 + 2 * (row - FULL_ROWS) if row < LAST_ROWS[0] else 24 + 2 * (row - LAST_ROWS[1])
    return 4 * (run_start + column - 1) + 3


def tile_successiveswintransfomerblock_pa_kernel(
    tc, x_mid, g3, b3, Wqkv2, bqkv2, out_0, out_1, out_2
):
    nc = tc.nc
    outs = [out_0, out_1, out_2]

    with ExitStack() as stack:
        keep = stack.enter_context(tc.tile_pool(name="keep", bufs=1))
        small = stack.enter_context(tc.tile_pool(name="small", bufs=3))
        z_pool = stack.enter_context(tc.tile_pool(name="z_pool", bufs=6))
        round_pool = stack.enter_context(tc.tile_pool(name="round_pool", bufs=3))
        w_pool = stack.enter_context(tc.tile_pool(name="w_pool", bufs=2 * PASSES))
        wg_pool = stack.enter_context(tc.tile_pool(name="wg_pool", bufs=4))
        stage_pool = stack.enter_context(tc.tile_pool(name="stage_pool", bufs=3))
        last_pool = stack.enter_context(tc.tile_pool(name="last_pool", bufs=2))
        psum = stack.enter_context(tc.psum_pool(name="psum", bufs=4))

        x_rows = x_mid.rearrange("b (r c) k -> (b r) c k", c=SIDE)
        x_main = keep.tile([P, WINDOW, D], BF16)
        x_last = keep.tile([P, D], BF16)

        def load_columns(j0, j1):
            groups = [(0, FULL_ROWS, column) for column in range(GRID)]
            groups.append((FULL_ROWS, IMAGES * SIDE, 0))
            for row0, row1, column in groups:
                c0 = (column * WINDOW + j0 - SHIFT) % SIDE
                nc.sync.dma_start(
                    out=x_main[home(row0, column) : home(row1 - 1, column) + 1 : 4, j0:j1, :]
                    .rearrange("p j k -> p (j k)"),
                    in_=x_rows[row0:row1, c0 : c0 + j1 - j0, :].rearrange("r c k -> r (c k)"),
                )
            for row0 in (LAST_ROWS[0] - RUN, LAST_ROWS[1]):
                inner = x_rows[row0 : row0 + RUN, SHIFT : SHIFT + 2 * WINDOW, :].rearrange(
                    "r (w j) k -> r w j k", w=2
                )
                nc.sync.dma_start(
                    out=x_main[home(row0, 1) : home(row0 + RUN - 1, 2) + 1 : 4, j0:j1, :]
                    .rearrange("p j k -> p (j k)"),
                    in_=inner[:, :, j0:j1, :].rearrange("r w j k -> r w (j k)"),
                )

        w_rows = Wqkv2.rearrange("(c t p) n -> c p t n", t=PACK, p=P)
        w_raw = {}

        def load_weights(first, count):
            for c in range(PASSES):
                raw = w_pool.tile([P, PACK, D], BF16, name="w_raw")
                nc.sync.dma_start(out=raw[:], in_=w_rows[c][:, :, first * D : (first + count) * D])
                for n in range(count):
                    w_raw[(first + n, c)] = raw[:, :, n * D : (n + 1) * D]

        bias_rows = keep.tile([P, TENSORS * D], BF16)
        nc.vector.memset(bias_rows[:].bitcast(mybir.dt.int32), 0)
        gb_rows = keep.tile([P, P], BF16)
        nc.vector.memset(gb_rows[:], 0.0)

        columns_in_order = [4, 5, 6, 7, 0, 1, 2, 3]
        def load_vectors():
            nc.sync.dma_start(out=bias_rows[0:1, :], in_=bqkv2.rearrange("(o n) -> o n", o=1))
            nc.sync.dma_start(out=gb_rows[0:K_BLOCKS, :], in_=g3.rearrange("(r c) -> r c", c=P))
            nc.sync.dma_start(
                out=gb_rows[K_BLOCKS : 2 * K_BLOCKS, :], in_=b3.rearrange("(r c) -> r c", c=P)
            )

        def load_last():
            nc.sync.dma_start(
                out=x_last[:], in_=x_rows[LAST_ROWS[0] : LAST_ROWS[1], SHIFT : SHIFT + 2 * WINDOW, :]
            )
        x_tiles = [x_main[:, j, :] for j in columns_in_order] + [x_last[:]]
        LAST = WINDOW

        ident = keep.tile([P, P], F32)
        make_identity(nc, ident[:])
        sort_main = keep.tile([P, P], F32)
        for row in range(0, IMAGES * SIDE, RUN):
            image, r0 = divmod(row, SIDE)
            window_row, i0 = divmod((r0 + SHIFT) % SIDE, WINDOW)
            window = image * POSITIONS + window_row * GRID
            columns = GRID if row < FULL_ROWS else 1
            first = 4 * (row % FULL_ROWS)
            lane = slice(0, GRID) if row < FULL_ROWS else slice(3, 4)
            nc.vector.tensor_copy(
                out=sort_main[:, window * WINDOW : (window + columns) * WINDOW]
                .rearrange("p (w i) -> p w i", w=columns)[:, :, i0 : i0 + RUN],
                in_=ident[:, first : first + 4 * RUN].rearrange("p (i c) -> p c i", c=4)[:, lane, :],
            )
            if row >= FULL_ROWS and window + 2 < MAIN_WINDOWS:
                first = home(row, 1) - 3
                nc.vector.tensor_copy(
                    out=sort_main[:, (window + 1) * WINDOW : (window + 3) * WINDOW]
                    .rearrange("p (w i) -> p w i", w=2)[:, :, i0 : i0 + RUN],
                    in_=ident[:, first : first + 8 * RUN]
                    .rearrange("p (i w c) -> p w i c", w=2, c=4)[:, :, :, 3],
                )
        sort_last = keep.tile([P, P], F32)
        nc.vector.tensor_copy(
            out=sort_last[:].rearrange("p (i j w) -> p i j w", i=WINDOW, w=LAST_WINDOWS),
            in_=ident[:].rearrange("p (i w j) -> p i j w", i=WINDOW, w=LAST_WINDOWS),
        )
        sorts = [sort_main] * WINDOW + [sort_last]
        gb_cols = keep.tile([P, 2 * K_BLOCKS], F32)

        def gain_and_bias():
            gb_rows_f32 = keep.tile([P, P], F32)
            nc.vector.tensor_copy(out=gb_rows_f32[:], in_=gb_rows[:])
            gb_bank = psum.tile([P, N_TILE], F32, tag="flip")
            nc.tensor.transpose(out=gb_bank[:, 0:P], in_=gb_rows_f32[:], identity=ident[:])
            nc.vector.tensor_copy(out=gb_cols[:], in_=gb_bank[:, 0 : 2 * K_BLOCKS])

        ones = keep.tile([P, P], BF16)
        nc.vector.memset(ones[:], 1.0)
        bias_bc = keep.tile([P, TENSORS * D], BF16)

        def spread_bias(n):
            cols = slice(n * N_TILE, (n + 1) * N_TILE)
            bank = psum.tile([P, N_TILE], F32, name="acc", tag="acc")
            nc.tensor.matmul(out=bank[:], lhsT=ones[:], rhs=bias_rows[:, cols], start=True, stop=True)
            nc.scalar.copy(out=bias_bc[:, cols], in_=bank[:])

        mean_var = keep.tile([P, TOKEN_TILES, 2], F32)
        std = keep.tile([P, TOKEN_TILES], F32)
        rstd = keep.tile([P, TOKEN_TILES], F32)
        x_codes = keep.tile([P, PASSES, TOKEN_TILES * P], U32, align_bytes=64)
        x_scales = keep.tile([P, PASSES, TOKEN_TILES * P], U8, align_bytes=64)

        stats_of = {}

        def bh(a, h):
            if h == 0:
                stats_of[a] = small.tile([P, D // STATS_CHUNK, 6], F32, name="stats")
            nc.vector.bn_stats(
                out=stats_of[a][:, h, :], in_=x_tiles[a][:, h * STATS_CHUNK : (h + 1) * STATS_CHUNK]
            )

        def ag(a):
            nc.vector.bn_aggr(
                out=mean_var[:, a, :], in_=stats_of[a][:].rearrange("p h s -> p (h s)")
            )

        def vector_statistics(a):
            bh(a, 0)
            bh(a, 1)
            ag(a)

        minus_half = keep.tile([P, TOKEN_TILES], F32)
        nc.gpsimd.memset(minus_half[:], -0.5)

        def inverse_deviation(tiles):
            part = slice(tiles[0], tiles[-1] + 1)
            nc.gpsimd.tensor_scalar(
                out=std[:, part], in0=mean_var[:, part, 1], scalar1=LN_EPS, scalar2=None, op0=ALU.add
            )
            nc.gpsimd.tensor_tensor(
                out=rstd[:, part], in0=std[:, part], in1=minus_half[:, part], op=ALU.pow
            )

        z_tiles = {}

        def centre(a):
            z = z_pool.tile([P, D], F32, name="z")
            nc.vector.tensor_scalar(
                out=z[:], in0=x_tiles[a],
                scalar1=mean_var[:, a, 0:1], scalar2=rstd[:, a : a + 1],
                op0=ALU.subtract, op1=ALU.mult,
            )
            z_tiles[a] = z

        shift = keep.tile([P, TOKEN_TILES], F32)

        def centre_by_scalar(a):
            z = z_pool.tile([P, D], F32, name="z")
            nc.gpsimd.tensor_tensor(
                out=shift[:, a : a + 1], in0=mean_var[:, a, 0:1], in1=rstd[:, a : a + 1], op=ALU.mult
            )
            nc.gpsimd.tensor_scalar(
                out=shift[:, a : a + 1], in0=shift[:, a : a + 1], scalar1=-1.0, scalar2=None, op0=ALU.mult
            )
            nc.scalar.activation(
                out=z[:], in_=x_tiles[a], func=ACT.Identity,
                scale=rstd[:, a : a + 1], bias=shift[:, a : a + 1],
            )
            z_tiles[a] = z

        planes = {}

        def flip(tiles, c):
            width = len(tiles) * P
            plane = round_pool.tile([P, PACK, width], BF16, name="plane")
            for t in range(PACK):
                j = c * PACK + t
                bank = psum.tile([P, N_TILE], F32, name="flipped", tag="flip")
                for n, a in enumerate(tiles):
                    nc.tensor.transpose(
                        out=bank[:, n * P : (n + 1) * P],
                        in_=z_tiles[a][:, j * P : (j + 1) * P],
                        identity=sorts[a][:],
                    )
                nc.scalar.activation(
                    out=plane[:, t, :], in_=bank[:, 0:width],
                    func=ACT.Identity, scale=gb_cols[:, j : j + 1],
                    bias=gb_cols[:, K_BLOCKS + j : K_BLOCKS + j + 1],
                )
            planes[(tiles[0], c)] = plane

        x_grouped = {}

        def group(tiles, c):
            grouped = round_pool.tile([P, len(tiles) * P, PACK], BF16, name="grouped", align_bytes=64)
            nc.vector.tensor_copy(
                out=grouped[:].rearrange("p (n i) t -> p n t i", i=4),
                in_=planes[(tiles[0], c)][:].rearrange("p t (n i) -> p n t i", i=4),
            )
            x_grouped[(tiles[0], c)] = grouped

        def quantise(tiles, c):
            cols = slice(tiles[0] * P, (tiles[-1] + 1) * P)
            nc.vector.quantize_mx(
                out=x_codes[:, c, cols].bitcast(FP8X4),
                scales=x_scales[:, c, cols],
                in_=x_grouped[(tiles[0], c)][:].rearrange("p m t -> p (m t)"),
            )

        w_codes = keep.tile([P, PASSES, TENSORS * D], U32, align_bytes=64)
        w_scales = keep.tile([P, PASSES, TENSORS * D], U8, align_bytes=64)
        w_grouped = {}

        def group_weights(tensor, half, c, engine):
            rows = w_raw[(tensor, c)][:, :, half * N_TILE : (half + 1) * N_TILE]
            grouped = wg_pool.tile([P, N_TILE, PACK], BF16, name="w_group", align_bytes=64)
            side_by_side = grouped[:].rearrange("p (n i) t -> p n t i", i=4)
            rows = rows.rearrange("p t (n i) -> p n t i", i=4)
            if engine == "V":
                nc.vector.tensor_copy(out=side_by_side, in_=rows)
            elif engine == "G":
                nc.gpsimd.tensor_scalar(
                    out=side_by_side, in0=rows, scalar1=1.0, scalar2=0.0, op0=ALU.mult, op1=ALU.add
                )
            else:
                nc.scalar.copy(out=side_by_side, in_=rows)
            w_grouped[(tensor, half, c)] = grouped

        def quantise_weights(tensor, half, c):
            cols = slice(tensor * D + half * N_TILE, tensor * D + (half + 1) * N_TILE)
            nc.vector.quantize_mx(
                out=w_codes[:, c, cols].bitcast(FP8X4),
                scales=w_scales[:, c, cols],
                in_=w_grouped[(tensor, half, c)][:].rearrange("p n t -> p (n t)"),
            )

        def project(a, tensor, half):
            tokens = slice(a * P, (a + 1) * P)
            cols = slice(tensor * D + half * N_TILE, tensor * D + (half + 1) * N_TILE)
            acc = psum.tile([P, N_TILE], F32, name="acc", tag="acc")
            for c in range(PASSES):
                nc.tensor.matmul_mx(
                    out=acc[:],
                    lhsT=x_codes[:, c, tokens].bitcast(FP8X4),
                    lhsT_scale=x_scales[:, c, tokens],
                    rhs=w_codes[:, c, cols].bitcast(FP8X4),
                    rhs_scale=w_scales[:, c, cols],
                    start=(c == 0),
                    stop=(c == PASSES - 1),
                )
            return acc

        def empty(acc, tensor, half, target, by_scalar):
            cols = slice(tensor * D + half * N_TILE, tensor * D + (half + 1) * N_TILE)
            product = acc[:].rearrange("p (h d) -> p h d", d=HEAD_DIM)
            bias = bias_bc[:, cols].rearrange("p (h d) -> p h d", d=HEAD_DIM)
            if by_scalar:
                nc.scalar.copy(out=target, in_=product)
                nc.gpsimd.tensor_tensor(out=target, in0=target, in1=bias, op=ALU.add)
            else:
                nc.vector.tensor_tensor(out=target, in0=product, in1=bias, op=ALU.add)

        def store_last(tensor, stage):
            for w in range(LAST_WINDOWS):
                nc.sync.dma_start(
                    out=outs[tensor][MAIN_WINDOWS + w].rearrange("h n d -> n h d"),
                    in_=stage[w:P:LAST_WINDOWS],
                )

        def store_main(tensor, half, key, j0, j1):
            stage = stages[key]
            for h in range(BANK_HEADS):
                head = outs[tensor][0:MAIN_WINDOWS, half * BANK_HEADS + h, :, :].rearrange(
                    "w (i j) d -> w i j d", j=WINDOW
                )
                nc.sync.dma_start(
                    out=head[:, :, j0:j1, :].rearrange("w i j d -> w i (j d)"),
                    in_=stage[:, h, :, :].rearrange("p j d -> p (j d)"),
                )

        stages = {}

        A, B, C, E, L = [0, 1], [2, 3], [4, 5], [6, 7], [8]
        rs, ce, cs, fl, gr, qu = inverse_deviation, centre, centre_by_scalar, flip, group, quantise
        gw, qw, sb = group_weights, quantise_weights, spread_bias
        stack.enter_context(tc.manual_schedule())
        load_columns(4, 6)
        load_vectors()
        load_columns(6, 8)
        load_weights(0, 1)
        load_weights(1, 1)
        load_columns(0, 2)
        load_columns(2, 4)
        load_last()
        load_weights(2, 1)
        for n in range(6): sb(n)
        bh(0, 0); bh(0, 1); bh(1, 0); ag(0); bh(1, 1); bh(2, 0); ag(1); rs(A); gain_and_bias(); bh(2, 1)
        ce(0); cs(1); fl(A, 0); fl(A, 1)
        bh(3, 0); ag(2); bh(3, 1); ag(3); rs(B)
        gw(0, 0, 0, "V")
        gr(A, 0); ce(2); cs(3); fl(B, 0); fl(B, 1)
        gr(A, 1); qu(A, 0); gw(0, 0, 1, "V"); qu(A, 1)
        qw(0, 0, 0); qw(0, 0, 1)
        gr(B, 0); gr(B, 1); qu(B, 0); qu(B, 1)
        gw(0, 1, 0, "S")

        todo = [(n, t, h) for t in range(2) for h in range(2) for n in range(4)] + [(n, t, h) for t in range(2) for pair in ((4, 5), (6, 7)) for h in range(2) for n in pair] + [(8, t, h) for t in range(2) for h in range(2)] + [(n, 2, 0) for n in range(8)] + [(8, 2, 0), (8, 2, 1)] + [(n, 2, 1) for n in range(8)]
        background = {1: [(gw, 0, 1, 1, "V"), (gw, 1, 0, 0, "S")], 2: [(qw, 0, 1, 0)], 3: [(qw, 0, 1, 1), (gw, 1, 0, 1, "S")], 4: [(bh, 4, 0), (gw, 1, 1, 0, "S")], 5: [(bh, 4, 1)], 6: [(ag, 4), (qw, 1, 0, 0), (gw, 1, 1, 1, "S")], 7: [(qw, 1, 0, 1)], 8: [(bh, 5, 0)], 9: [(bh, 5, 1)], 10: [(ag, 5), (rs, C), (qw, 1, 1, 0)], 11: [(qw, 1, 1, 1), (bh, 6, 0)], 12: [(ce, 4), (cs, 5), (fl, C, 0), (fl, C, 1), (bh, 6, 1)], 13: [(bh, 7, 0), (ag, 6), (bh, 7, 1)], 14: [(ag, 7), (rs, E)], 15: [(gr, C, 0), (ce, 6), (cs, 7), (fl, E, 0), (fl, E, 1), (gr, C, 1), (qu, C, 0), (qu, C, 1)],
 18: [(gr, E, 0), (bh, 8, 0), (gr, E, 1), (qu, E, 0)], 19: [(qu, E, 1), (gw, 2, 0, 0, "S")], 21: [(bh, 8, 1), (gw, 2, 0, 1, "S")], 22: [(ag, 8), (rs, L)], 23: [(gw, 2, 1, 0, "S")], 24: [(ce, 8)], 25: [(gw, 2, 1, 1, "S"), (fl, L, 0), (fl, L, 1)], 26: [(qw, 2, 0, 0)], 28: [(qw, 2, 0, 1)], 29: [(gr, L, 0)], 30: [(gr, L, 1), (qu, L, 0)], 31: [(qu, L, 1)], 33: [(qw, 2, 1, 0)], 35: [(qw, 2, 1, 1)]}
        def target_of(n, t, h):
            if n == LAST:
                if (t, "last") not in stages:
                    stages[(t, "last")] = last_pool.tile([P, HEADS, HEAD_DIM], F32, name="stage_last")
                return stages[(t, "last")][:, h * BANK_HEADS : (h + 1) * BANK_HEADS, :]
            if t < 2:
                key = (t, h, n // 4)
                if key not in stages:
                    stages[key] = stage_pool.tile([P, BANK_HEADS, WINDOW // 2, HEAD_DIM], F32, name="part", bufs=4)
                return stages[key][:, :, n % 4, :]
            if (t, h) not in stages:
                stages[(t, h)] = stage_pool.tile([P, BANK_HEADS, WINDOW, HEAD_DIM], F32, name="stage", bufs=2)
            return stages[(t, h)][:, :, columns_in_order[n], :]
        open_banks = []
        left = {}
        for n, t, h in todo:
            key = (t, "last") if n == LAST else (t, h, n // 4) if t < 2 else (t, h)
            left[key] = left.get(key, 0) + 1
        def finish():
            n, t, h, acc = open_banks.pop(0)
            empty(acc, t, h, target_of(n, t, h), False)
            key = (t, "last") if n == LAST else (t, h, n // 4) if t < 2 else (t, h)
            left[key] -= 1
            if left[key] == 0:
                if n == LAST:
                    store_last(t, stages[key])
                elif t < 2:
                    j0 = columns_in_order[n // 4 * 4]
                    store_main(t, h, key, j0, j0 + 4)
                else:
                    store_main(t, h, key, 0, WINDOW)
        for i, (n, t, h) in enumerate(todo):
            open_banks.append((n, t, h, project(n, t, h)))
            for step in background.get(i, []):
                step[0](*step[1:])
            if len(open_banks) > 2: finish()
        while open_banks: finish()
